import numpy as np
import ml_dtypes


def mxq(x, axis, fmt="e4m3"):
    dtype, down = {"e4m3": (ml_dtypes.float8_e4m3fn, 7), "e5m2": (ml_dtypes.float8_e5m2, 14)}[fmt]
    v = np.moveaxis(np.asarray(x, np.float32).astype(ml_dtypes.bfloat16).astype(np.float64), axis, -1)
    blocks = v.reshape(v.shape[:-1] + (-1, 32))
    amax = np.abs(blocks).max(-1, keepdims=True)
    byte = np.maximum(np.where(amax > 0, np.frexp(amax)[1] - 1 + 127, 0) - down, 1)
    scale = np.exp2(byte - 127.0)
    codes = (blocks / scale).astype(np.float32).astype(dtype).astype(np.float64)
    return np.moveaxis((codes * scale).reshape(v.shape), -1, axis)


WIDE = False


def mx_kscale(k):
    if not WIDE:
        return np.ones(k)
    levels = np.array([10, -10, 5, -5, 0])
    a = np.random.permutation(np.resize(levels, k // 512 * 4)).reshape(k // 512, 4)
    idx = np.arange(k)
    return np.exp2(a[idx // 512, idx % 128 // 32])


BF16 = ml_dtypes.bfloat16


def bf(x):
    return np.asarray(x, np.float32).astype(BF16)


def f64(x):
    return np.asarray(x).astype(np.float64)


B, I, H = 512, 256, 1024


def setup_inputs():
    s = mx_kscale(H)
    w1 = np.concatenate([np.random.standard_normal((H, H)) * 1.5 / np.sqrt(H) / s, np.random.standard_normal(H)[:, None] * 0.6], axis=1)
    return {"h_tilde": bf(np.random.standard_normal((B, H)) * 0.3 * s),
            "k1": bf(np.random.standard_normal((B, H)) * 0.8 * s),
            "k2": bf(np.random.standard_normal((B, H)) * 1.0 * s),
            "k3": bf(np.random.standard_normal((B, H)) * 1.0 * s),
            "t0": bf(0.2 + 0.1 * np.random.random(1)),
            "t1": bf(1.0 + 0.2 * np.random.random(1)),
            "W1": bf(w1),
            "b1": bf(np.random.standard_normal(H) * 0.3),
            "W2": bf(np.random.standard_normal((H, H)) * 1.5 / np.sqrt(H) * s[:, None]),
            "b2": bf(np.random.standard_normal(H) * 0.3 * s)}


def reference(h_tilde, k1, k2, k3, t0, t1, W1, b1, W2, b2):
    dt = f64(t1) - f64(t0)
    t = f64(t0) + dt
    ht = f64(h_tilde)
    y = ht + dt * f64(k3)
    w1 = f64(W1)
    z = np.tanh((mxq(y, 1, "e4m3") @ mxq(w1[:, :H], 1, "e4m3").T) + t * w1[:, H] + f64(b1))
    k4 = (mxq(z, 1, "e4m3") @ mxq(f64(W2), 1, "e4m3").T) + f64(b2)
    return ht + (dt / 6.0) * (f64(k1) + 2.0 * f64(k2) + 2.0 * f64(k3) + k4)

@@ -1,0 +1,261 @@
+from contextlib import ExitStack
+
+import concourse.mybir as mybir
+from concourse.masks import make_identity
+
+F32 = mybir.dt.float32
+BF16 = mybir.dt.bfloat16
+U32 = mybir.dt.uint32
+U8 = mybir.dt.uint8
+FP8X4 = mybir.dt.float8_e4m3fn_x4
+ALU = mybir.AluOpType
+ACT = mybir.ActivationFunctionType
+
+P = 128
+B = 512
+H = 1024
+PACK = 4
+K_PASS = P * PACK
+PASSES = H // K_PASS
+ROW_BLOCKS = B // P
+CHUNKS = 4
+CHUNK_ROWS = H // CHUNKS
+BLOCKS_PER_CHUNK = CHUNK_ROWS // P
+WORDS = H // 2
+N_HALF = 512
+HALVES = H // N_HALF
+
+FLOPS = 2 * 2 * B * H * H
+
+
+def tile_nodelstmcell_pc_kernel(tc, h_tilde, k1, k2, k3, t0, t1, W1, b1, W2, b2, out):
+    nc = tc.nc
+    with ExitStack() as ctx:
+        const = ctx.enter_context(tc.tile_pool(name="const", bufs=1))
+        data = ctx.enter_context(tc.tile_pool(name="data", bufs=1))
+        weights = ctx.enter_context(tc.tile_pool(name="weights", bufs=CHUNKS))
+        stage = ctx.enter_context(tc.tile_pool(name="stage", bufs=3))
+        keep = ctx.enter_context(tc.tile_pool(name="keep", bufs=1))
+        psum = ctx.enter_context(tc.psum_pool(name="psum", bufs=2))
+
+        ident_f32 = const.tile([P, P], F32)
+        make_identity(nc, ident_f32[:])
+        ident_bf16 = const.tile([P, P], BF16)
+        make_identity(nc, ident_bf16[:])
+
+        t0_all = const.tile([P, 1], BF16)
+        t1_all = const.tile([P, 1], BF16)
+        nc.scalar.dma_start(out=t0_all[:], in_=t0.partition_broadcast(P))
+        nc.scalar.dma_start(out=t1_all[:], in_=t1.partition_broadcast(P))
+        warm_in = const.tile([P, 1], F32)
+        warm_out = const.tile([P, 1], F32)
+        nc.vector.memset(warm_in[:], 0.0)
+        nc.scalar.activation(out=warm_out[:], in_=warm_in[:], func=ACT.Tanh)
+
+        h_sb = data.tile([P, ROW_BLOCKS, H], BF16)
+        k1_sb = data.tile([P, ROW_BLOCKS, H], BF16)
+        k2_sb = data.tile([P, ROW_BLOCKS, H], BF16)
+        k3_sb = data.tile([P, ROW_BLOCKS, H], BF16)
+        h_rows = h_tilde.rearrange("(r p) j -> p r j", p=P)
+        k1_rows = k1.rearrange("(r p) j -> p r j", p=P)
+        k2_rows = k2.rearrange("(r p) j -> p r j", p=P)
+        k3_rows = k3.rearrange("(r p) j -> p r j", p=P)
+        out_rows = out.rearrange("(r p) j -> p r j", p=P)
+
+        for r in range(ROW_BLOCKS):
+            nc.sync.dma_start(out=h_sb[:, r, :], in_=h_rows[:, r, :])
+            nc.sync.dma_start(out=k3_sb[:, r, :], in_=k3_rows[:, r, :])
+        for r in range(ROW_BLOCKS):
+            nc.sync.dma_start(out=k2_sb[:, r, :], in_=k2_rows[:, r, :])
+
+        b1_cols = const.tile([P, CHUNKS, BLOCKS_PER_CHUNK], BF16)
+        b2_cols = const.tile([P, H // P], BF16)
+        with nc.allow_non_contiguous_dma(reason="two bias vectors of 2 KiB, one value to a partition"):
+            nc.sync.dma_start(out=b1_cols[:], in_=b1.rearrange("(c p e) -> p c e", p=P, e=BLOCKS_PER_CHUNK))
+            nc.sync.dma_start(out=b2_cols[:], in_=b2.rearrange("(s p) -> p s", p=P))
+
+        w1_view = W1.rearrange("(c p e) k -> c p e k", p=P, e=BLOCKS_PER_CHUNK)
+        w1_chunks = []
+        for c in range(CHUNKS):
+            w1_c = weights.tile([P, BLOCKS_PER_CHUNK, H + 2], BF16)
+            nc.sync.dma_start(out=w1_c[:, :, 0 : H + 1], in_=w1_view[c])
+            w1_chunks.append(w1_c)
+        for r in range(ROW_BLOCKS):
+            nc.sync.dma_start(out=k1_sb[:, r, :], in_=k1_rows[:, r, :])
+        w2_view = W2.rearrange("(c s p) k -> c p s k", s=BLOCKS_PER_CHUNK, p=P)
+        w2_chunks = []
+        for c in range(CHUNKS):
+            w2_c = weights.tile([P, BLOCKS_PER_CHUNK, H], BF16)
+            nc.sync.dma_start(out=w2_c[:], in_=w2_view[c])
+            w2_chunks.append(w2_c)
+
+        dt = const.tile([P, 1], F32)
+        t_end = const.tile([P, 1], F32)
+        dt_sixth = const.tile([P, 1], F32)
+        nc.vector.tensor_tensor(out=dt[:], in0=t1_all[:], in1=t0_all[:], op=ALU.subtract)
+        nc.vector.tensor_tensor(out=t_end[:], in0=t0_all[:], in1=dt[:], op=ALU.add)
+        nc.vector.tensor_scalar_mul(out=dt_sixth[:], in0=dt[:], scalar1=1.0 / 6.0)
+
+        y_split = keep.tile([P, ROW_BLOCKS, 2, WORDS], BF16)
+        y_grouped = keep.tile([P, PASSES, B, PACK], BF16, align_bytes=64)
+        y_codes = keep.tile([P, PASSES, B], U32, align_bytes=64)
+        y_scales = keep.tile([P, PASSES, B], U8, align_bytes=64)
+        for r in range(ROW_BLOCKS):
+            nc.vector.scalar_tensor_tensor(
+                out=y_split[:, r, :, :],
+                in0=k3_sb[:, r, :].rearrange("p (w e) -> p e w", e=2),
+                scalar=dt[:, 0:1],
+                in1=h_sb[:, r, :].rearrange("p (w e) -> p e w", e=2),
+                op0=ALU.mult,
+                op1=ALU.add,
+            )
+            y_t = psum.tile([P, PASSES, PACK, P], BF16, tag="tp")
+            for g in range(PASSES):
+                for u in range(2):
+                    for e in range(2):
+                        first = (2 * g + u) * P
+                        nc.tensor.transpose(
+                            out=y_t[:, g, 2 * u + e, :],
+                            in_=y_split[:, r, e, first : first + P],
+                            identity=ident_bf16[:],
+                        )
+            nc.scalar.copy(
+                out=y_grouped[:, :, r * P : (r + 1) * P, :],
+                in_=y_t[:].rearrange("p g t b -> p g b t"),
+            )
+
+        base = keep.tile([P, ROW_BLOCKS, H], F32)
+        for r in range(ROW_BLOCKS):
+            nc.vector.tensor_tensor(out=base[:, r, :], in0=k2_sb[:, r, :], in1=k3_sb[:, r, :], op=ALU.add)
+
+        nc.vector.quantize_mx(
+            out=y_codes[:].rearrange("p g b -> p (g b)").bitcast(FP8X4),
+            scales=y_scales[:].rearrange("p g b -> p (g b)"),
+            in_=y_grouped[:].rearrange("p g b t -> p (g b t)"),
+        )
+
+        def quantise_weight_chunk(w_chunk, codes, scales):
+            w_words = w_chunk[:].bitcast(F32)
+            grouped = stage.tile([P, PASSES, CHUNK_ROWS * PACK], BF16, align_bytes=64)
+            for g in range(PASSES):
+                w_t = psum.tile([P, 2, CHUNK_ROWS], F32, tag="tp")
+                for u in range(2):
+                    for s in range(BLOCKS_PER_CHUNK):
+                        first = (2 * g + u) * P
+                        nc.tensor.transpose(
+                            out=w_t[:, u, s * P : (s + 1) * P],
+                            in_=w_words[:, s, first : first + P],
+                            identity=ident_f32[:],
+                        )
+                nc.scalar.copy(
+                    out=grouped[:, g, :].bitcast(F32).rearrange("p (c u) -> p c u", u=2),
+                    in_=w_t[:].rearrange("p u c -> p c u"),
+                )
+            nc.vector.quantize_mx(
+                out=codes.bitcast(FP8X4),
+                scales=scales,
+                in_=grouped[:].rearrange("p g x -> p (g x)"),
+            )
+
+        w1_codes = keep.tile([P, CHUNKS, PASSES * CHUNK_ROWS], U32, align_bytes=64)
+        w1_scales = keep.tile([P, CHUNKS, PASSES * CHUNK_ROWS], U8, align_bytes=64)
+        bias1 = const.tile([P, CHUNKS, BLOCKS_PER_CHUNK], F32)
+        z_sb = keep.tile([P, H // P, B], BF16)
+        for c in range(CHUNKS):
+            quantise_weight_chunk(w1_chunks[c], w1_codes[:, c, :], w1_scales[:, c, :])
+            nc.vector.scalar_tensor_tensor(
+                out=bias1[:, c, :],
+                in0=w1_chunks[c][:, :, H],
+                scalar=t_end[:, 0:1],
+                in1=b1_cols[:, c, :],
+                op0=ALU.mult,
+                op1=ALU.add,
+            )
+            nc.vector.scalar_tensor_tensor(
+                out=base[:, c, :], in0=base[:, c, :], scalar=2.0, in1=k1_sb[:, c, :], op0=ALU.mult, op1=ALU.add
+            )
+            for e in range(BLOCKS_PER_CHUNK):
+                acc = psum.tile([P, B], F32, tag="acc")
+                for g in range(PASSES):
+                    cols = slice(g * CHUNK_ROWS + e * P, g * CHUNK_ROWS + (e + 1) * P)
+                    nc.tensor.matmul_mx(
+                        out=acc[:],
+                        lhsT=w1_codes[:, c, cols].bitcast(FP8X4),
+                        lhsT_scale=w1_scales[:, c, cols],
+                        rhs=y_codes[:, g, :].bitcast(FP8X4),
+                        rhs_scale=y_scales[:, g, :],
+                        start=(g == 0),
+                        stop=(g == PASSES - 1),
+                    )
+                nc.scalar.activation(
+                    out=z_sb[:, BLOCKS_PER_CHUNK * c + e, :],
+                    in_=acc[:],
+                    func=ACT.Tanh,
+                    bias=bias1[:, c, e : e + 1],
+                    scale=1.0,
+                )
+
+        z_grouped = keep.tile([P, PASSES, B * PACK], BF16, align_bytes=64)
+        z_codes = keep.tile([P, PASSES, B], U32, align_bytes=64)
+        z_scales = keep.tile([P, PASSES, B], U8, align_bytes=64)
+        for g in range(PASSES):
+            nc.scalar.copy(
+                out=z_grouped[:, g, :].rearrange("p (b t) -> p b t", t=PACK),
+                in_=z_sb[:, PACK * g : PACK * (g + 1), :].rearrange("p t b -> p b t"),
+            )
+            nc.vector.quantize_mx(
+                out=z_codes[:, g, :].bitcast(FP8X4), scales=z_scales[:, g, :], in_=z_grouped[:, g, :]
+            )
+
+        w2_codes = keep.tile([P, CHUNKS, PASSES * CHUNK_ROWS], U32, align_bytes=64)
+        w2_scales = keep.tile([P, CHUNKS, PASSES * CHUNK_ROWS], U8, align_bytes=64)
+        b2_scaled = const.tile([P, H // P], F32)
+        nc.vector.tensor_scalar_mul(out=b2_scaled[:], in0=b2_cols[:], scalar1=dt_sixth[:, 0:1])
+        for c in range(CHUNKS):
+            quantise_weight_chunk(w2_chunks[c], w2_codes[:, c, :], w2_scales[:, c, :])
+            nc.vector.scalar_tensor_tensor(
+                out=base[:, c, :],
+                in0=base[:, c, :],
+                scalar=dt_sixth[:, 0:1],
+                in1=h_sb[:, c, :],
+                op0=ALU.mult,
+                op1=ALU.add,
+            )
+
+        tiles_per_half = N_HALF // P
+        for half in range(HALVES):
+            k4_t = stage.tile([P, tiles_per_half, B], F32)
+            for s in range(tiles_per_half):
+                tile_index = half * tiles_per_half + s
+                c = tile_index // BLOCKS_PER_CHUNK
+                e = tile_index % BLOCKS_PER_CHUNK
+                acc = psum.tile([P, B], F32, tag="acc")
+                for g in range(PASSES):
+                    cols = slice(g * CHUNK_ROWS + e * P, g * CHUNK_ROWS + (e + 1) * P)
+                    nc.tensor.matmul_mx(
+                        out=acc[:],
+                        lhsT=w2_codes[:, c, cols].bitcast(FP8X4),
+                        lhsT_scale=w2_scales[:, c, cols],
+                        rhs=z_codes[:, g, :].bitcast(FP8X4),
+                        rhs_scale=z_scales[:, g, :],
+                        start=(g == 0),
+                        stop=(g == PASSES - 1),
+                    )
+                nc.scalar.activation(
+                    out=k4_t[:, s, :],
+                    in_=acc[:],
+                    func=ACT.Identity,
+                    bias=b2_scaled[:, tile_index : tile_index + 1],
+                    scale=dt_sixth[:, 0:1],
+                )
+            for r in range(ROW_BLOCKS):
+                back = psum.tile([P, N_HALF], F32, tag="back", bufs=ROW_BLOCKS)
+                for s in range(tiles_per_half):
+                    nc.tensor.transpose(
+                        out=back[:, s * P : (s + 1) * P],
+                        in_=k4_t[:, s, r * P : (r + 1) * P],
+                        identity=ident_f32[:],
+                    )
+                cols = slice(half * N_HALF, (half + 1) * N_HALF)
+                nc.vector.tensor_tensor(out=base[:, r, cols], in0=back[:], in1=base[:, r, cols], op=ALU.add)
+                nc.sync.dma_start(out=out_rows[:, r, cols], in_=base[:, r, cols])

@@ -20,17 +20,24 @@ PASSES = H // K_PASS
 ROW_BLOCKS = B // P
 CHUNKS = 4
 CHUNK_ROWS = H // CHUNKS
-BLOCKS_PER_CHUNK = CHUNK_ROWS // P
+TILES_PER_CHUNK = CHUNK_ROWS // P
 WORDS = H // 2
 N_HALF = 512
 HALVES = H // N_HALF
+TILES_PER_HALF = N_HALF // P
+QUANTISE_LAG = 1
+LAYER_LAG = 2
+Z_LAG = 3
 
 FLOPS = 2 * 2 * B * H * H
 
 
 def tile_nodelstmcell_pc_kernel(tc, h_tilde, k1, k2, k3, t0, t1, W1, b1, W2, b2, out):
     nc = tc.nc
+    left = slice(0, N_HALF)
+    right = slice(N_HALF, H)
     with ExitStack() as ctx:
+        ctx.enter_context(tc.manual_schedule())
         const = ctx.enter_context(tc.tile_pool(name="const", bufs=1))
         data = ctx.enter_context(tc.tile_pool(name="data", bufs=1))
         weights = ctx.enter_context(tc.tile_pool(name="weights", bufs=CHUNKS))
@@ -38,19 +45,10 @@ def tile_nodelstmcell_pc_kernel(tc, h_tilde, k1, k2, k3, t0, t1, W1, b1, W2, b2,
         keep = ctx.enter_context(tc.tile_pool(name="keep", bufs=1))
         psum = ctx.enter_context(tc.psum_pool(name="psum", bufs=2))
 
-        ident_f32 = const.tile([P, P], F32)
-        make_identity(nc, ident_f32[:])
-        ident_bf16 = const.tile([P, P], BF16)
-        make_identity(nc, ident_bf16[:])
-
         t0_all = const.tile([P, 1], BF16)
         t1_all = const.tile([P, 1], BF16)
         nc.scalar.dma_start(out=t0_all[:], in_=t0.partition_broadcast(P))
         nc.scalar.dma_start(out=t1_all[:], in_=t1.partition_broadcast(P))
-        warm_in = const.tile([P, 1], F32)
-        warm_out = const.tile([P, 1], F32)
-        nc.vector.memset(warm_in[:], 0.0)
-        nc.scalar.activation(out=warm_out[:], in_=warm_in[:], func=ACT.Tanh)
 
         h_sb = data.tile([P, ROW_BLOCKS, H], BF16)
         k1_sb = data.tile([P, ROW_BLOCKS, H], BF16)
@@ -61,33 +59,40 @@ def tile_nodelstmcell_pc_kernel(tc, h_tilde, k1, k2, k3, t0, t1, W1, b1, W2, b2,
         k2_rows = k2.rearrange("(r p) j -> p r j", p=P)
         k3_rows = k3.rearrange("(r p) j -> p r j", p=P)
         out_rows = out.rearrange("(r p) j -> p r j", p=P)
+        b1_cols = const.tile([P, CHUNKS, TILES_PER_CHUNK], BF16)
+        b2_cols = const.tile([P, H // P], BF16)
+        w1_view = W1.rearrange("(c p e) k -> c p e k", p=P, e=TILES_PER_CHUNK)
+        w2_view = W2.rearrange("(c s p) k -> c p s k", s=TILES_PER_CHUNK, p=P)
 
         for r in range(ROW_BLOCKS):
             nc.sync.dma_start(out=h_sb[:, r, :], in_=h_rows[:, r, :])
             nc.sync.dma_start(out=k3_sb[:, r, :], in_=k3_rows[:, r, :])
-        for r in range(ROW_BLOCKS):
-            nc.sync.dma_start(out=k2_sb[:, r, :], in_=k2_rows[:, r, :])
-
-        b1_cols = const.tile([P, CHUNKS, BLOCKS_PER_CHUNK], BF16)
-        b2_cols = const.tile([P, H // P], BF16)
-        with nc.allow_non_contiguous_dma(reason="two bias vectors of 2 KiB, one value to a partition"):
-            nc.sync.dma_start(out=b1_cols[:], in_=b1.rearrange("(c p e) -> p c e", p=P, e=BLOCKS_PER_CHUNK))
+        with nc.allow_non_contiguous_dma(reason="a bias vector of 2 KiB, two values to a partition"):
+            nc.sync.dma_start(out=b1_cols[:], in_=b1.rearrange("(c p e) -> p c e", p=P, e=TILES_PER_CHUNK))
+        chunk_tiles = []
+        for c in range(CHUNKS):
+            w1_c = weights.tile([P, TILES_PER_CHUNK, H + 2], BF16)
+            nc.sync.dma_start(out=w1_c[:, :, 0 : H + 1], in_=w1_view[c])
+            chunk_tiles.append(w1_c)
+            nc.sync.dma_start(out=k2_sb[:, c, :], in_=k2_rows[:, c, :])
+            nc.sync.dma_start(out=k1_sb[:, c, :], in_=k1_rows[:, c, :])
+        for c in range(CHUNKS):
+            w2_c = weights.tile([P, TILES_PER_CHUNK, H], BF16)
+            nc.sync.dma_start(out=w2_c[:], in_=w2_view[c])
+            chunk_tiles.append(w2_c)
+        with nc.allow_non_contiguous_dma(reason="a bias vector of 2 KiB, one value to a partition"):
             nc.sync.dma_start(out=b2_cols[:], in_=b2.rearrange("(s p) -> p s", p=P))
 
-        w1_view = W1.rearrange("(c p e) k -> c p e k", p=P, e=BLOCKS_PER_CHUNK)
-        w1_chunks = []
-        for c in range(CHUNKS):
-            w1_c = weights.tile([P, BLOCKS_PER_CHUNK, H + 2], BF16)
-            nc.sync.dma_start(out=w1_c[:, :, 0 : H + 1], in_=w1_view[c])
-            w1_chunks.append(w1_c)
-        for r in range(ROW_BLOCKS):
-            nc.sync.dma_start(out=k1_sb[:, r, :], in_=k1_rows[:, r, :])
-        w2_view = W2.rearrange("(c s p) k -> c p s k", s=BLOCKS_PER_CHUNK, p=P)
-        w2_chunks = []
-        for c in range(CHUNKS):
-            w2_c = weights.tile([P, BLOCKS_PER_CHUNK, H], BF16)
-            nc.sync.dma_start(out=w2_c[:], in_=w2_view[c])
-            w2_chunks.append(w2_c)
+        ident_f32 = const.tile([P, P], F32)
+        make_identity(nc, ident_f32[:])
+        ident_bf16 = const.tile([P, P], BF16)
+        make_identity(nc, ident_bf16[:])
+        warm_in = const.tile([P, 1], F32)
+        warm_out = const.tile([P, 1], F32)
+        nc.vector.memset(warm_in[:], 0.0)
+        nc.scalar.activation(out=warm_out[:], in_=warm_in[:], func=ACT.Tanh)
+        twice_ident = const.tile([P, P], BF16)
+        nc.vector.tensor_scalar_mul(out=twice_ident[:], in0=ident_bf16[:], scalar1=2.0)
 
         dt = const.tile([P, 1], F32)
         t_end = const.tile([P, 1], F32)
@@ -123,24 +128,31 @@ def tile_nodelstmcell_pc_kernel(tc, h_tilde, k1, k2, k3, t0, t1, W1, b1, W2, b2,
                 out=y_grouped[:, :, r * P : (r + 1) * P, :],
                 in_=y_t[:].rearrange("p g t b -> p g b t"),
             )
-
-        base = keep.tile([P, ROW_BLOCKS, H], F32)
-        for r in range(ROW_BLOCKS):
-            nc.vector.tensor_tensor(out=base[:, r, :], in0=k2_sb[:, r, :], in1=k3_sb[:, r, :], op=ALU.add)
-
         nc.vector.quantize_mx(
             out=y_codes[:].rearrange("p g b -> p (g b)").bitcast(FP8X4),
             scales=y_scales[:].rearrange("p g b -> p (g b)"),
             in_=y_grouped[:].rearrange("p g b t -> p (g b t)"),
         )
 
-        def quantise_weight_chunk(w_chunk, codes, scales):
-            w_words = w_chunk[:].bitcast(F32)
+        w_codes = keep.tile([P, 2 * CHUNKS, PASSES * CHUNK_ROWS], U32, align_bytes=64)
+        w_scales = keep.tile([P, 2 * CHUNKS, PASSES * CHUNK_ROWS], U8, align_bytes=64)
+        bias1 = const.tile([P, CHUNKS, TILES_PER_CHUNK], F32)
+        b2_scaled = const.tile([P, H // P], F32)
+        z_sb = keep.tile([P, H // P, B], BF16)
+        z_grouped = keep.tile([P, PASSES, B * PACK], BF16, align_bytes=64)
+        z_codes = keep.tile([P, PASSES, B], U32, align_bytes=64)
+        z_scales = keep.tile([P, PASSES, B], U8, align_bytes=64)
+        base = keep.tile([P, ROW_BLOCKS, H], F32)
+        grouped_tiles = []
+        slope_sums = []
+
+        def transpose_chunk(i):
+            w_words = chunk_tiles[i][:].bitcast(F32)
             grouped = stage.tile([P, PASSES, CHUNK_ROWS * PACK], BF16, align_bytes=64)
             for g in range(PASSES):
                 w_t = psum.tile([P, 2, CHUNK_ROWS], F32, tag="tp")
                 for u in range(2):
-                    for s in range(BLOCKS_PER_CHUNK):
+                    for s in range(TILES_PER_CHUNK):
                         first = (2 * g + u) * P
                         nc.tensor.transpose(
                             out=w_t[:, u, s * P : (s + 1) * P],
@@ -151,96 +163,117 @@ def tile_nodelstmcell_pc_kernel(tc, h_tilde, k1, k2, k3, t0, t1, W1, b1, W2, b2,
                     out=grouped[:, g, :].bitcast(F32).rearrange("p (c u) -> p c u", u=2),
                     in_=w_t[:].rearrange("p u c -> p c u"),
                 )
+            grouped_tiles.append(grouped)
+
+        def quantise_chunk(i):
             nc.vector.quantize_mx(
-                out=codes.bitcast(FP8X4),
-                scales=scales,
-                in_=grouped[:].rearrange("p g x -> p (g x)"),
+                out=w_codes[:, i, :].bitcast(FP8X4),
+                scales=w_scales[:, i, :],
+                in_=grouped_tiles[i][:].rearrange("p g x -> p (g x)"),
             )
 
-        w1_codes = keep.tile([P, CHUNKS, PASSES * CHUNK_ROWS], U32, align_bytes=64)
-        w1_scales = keep.tile([P, CHUNKS, PASSES * CHUNK_ROWS], U8, align_bytes=64)
-        bias1 = const.tile([P, CHUNKS, BLOCKS_PER_CHUNK], F32)
-        z_sb = keep.tile([P, H // P, B], BF16)
-        for c in range(CHUNKS):
-            quantise_weight_chunk(w1_chunks[c], w1_codes[:, c, :], w1_scales[:, c, :])
+        def weights_times(i, s, moving_codes, moving_scales):
+            acc = psum.tile([P, B], F32, tag="acc")
+            for g in range(PASSES):
+                cols = slice(g * CHUNK_ROWS + s * P, g * CHUNK_ROWS + (s + 1) * P)
+                nc.tensor.matmul_mx(
+                    out=acc[:],
+                    lhsT=w_codes[:, i, cols].bitcast(FP8X4),
+                    lhsT_scale=w_scales[:, i, cols],
+                    rhs=moving_codes[:, g, :].bitcast(FP8X4),
+                    rhs_scale=moving_scales[:, g, :],
+                    start=(g == 0),
+                    stop=(g == PASSES - 1),
+                )
+            return acc
+
+        def first_layer(c):
             nc.vector.scalar_tensor_tensor(
                 out=bias1[:, c, :],
-                in0=w1_chunks[c][:, :, H],
+                in0=chunk_tiles[c][:, :, H],
                 scalar=t_end[:, 0:1],
                 in1=b1_cols[:, c, :],
                 op0=ALU.mult,
                 op1=ALU.add,
             )
-            nc.vector.scalar_tensor_tensor(
-                out=base[:, c, :], in0=base[:, c, :], scalar=2.0, in1=k1_sb[:, c, :], op0=ALU.mult, op1=ALU.add
-            )
-            for e in range(BLOCKS_PER_CHUNK):
-                acc = psum.tile([P, B], F32, tag="acc")
-                for g in range(PASSES):
-                    cols = slice(g * CHUNK_ROWS + e * P, g * CHUNK_ROWS + (e + 1) * P)
-                    nc.tensor.matmul_mx(
-                        out=acc[:],
-                        lhsT=w1_codes[:, c, cols].bitcast(FP8X4),
-                        lhsT_scale=w1_scales[:, c, cols],
-                        rhs=y_codes[:, g, :].bitcast(FP8X4),
-                        rhs_scale=y_scales[:, g, :],
-                        start=(g == 0),
-                        stop=(g == PASSES - 1),
-                    )
+            for e in range(TILES_PER_CHUNK):
+                acc = weights_times(c, e, y_codes, y_scales)
                 nc.scalar.activation(
-                    out=z_sb[:, BLOCKS_PER_CHUNK * c + e, :],
+                    out=z_sb[:, TILES_PER_CHUNK * c + e, :],
                     in_=acc[:],
                     func=ACT.Tanh,
                     bias=bias1[:, c, e : e + 1],
                     scale=1.0,
                 )
 
-        z_grouped = keep.tile([P, PASSES, B * PACK], BF16, align_bytes=64)
-        z_codes = keep.tile([P, PASSES, B], U32, align_bytes=64)
-        z_scales = keep.tile([P, PASSES, B], U8, align_bytes=64)
-        for g in range(PASSES):
-            nc.scalar.copy(
-                out=z_grouped[:, g, :].rearrange("p (b t) -> p b t", t=PACK),
-                in_=z_sb[:, PACK * g : PACK * (g + 1), :].rearrange("p t b -> p b t"),
+        def quantise_z(g):
+            nc.vector.tensor_copy(
+                out=z_grouped[:, g, :].rearrange("p (c i t) -> p c t i", i=4, t=PACK),
+                in_=z_sb[:, PACK * g : PACK * (g + 1), :].rearrange("p t (c i) -> p c t i", i=4),
             )
             nc.vector.quantize_mx(
                 out=z_codes[:, g, :].bitcast(FP8X4), scales=z_scales[:, g, :], in_=z_grouped[:, g, :]
             )
 
-        w2_codes = keep.tile([P, CHUNKS, PASSES * CHUNK_ROWS], U32, align_bytes=64)
-        w2_scales = keep.tile([P, CHUNKS, PASSES * CHUNK_ROWS], U8, align_bytes=64)
-        b2_scaled = const.tile([P, H // P], F32)
-        nc.vector.tensor_scalar_mul(out=b2_scaled[:], in0=b2_cols[:], scalar1=dt_sixth[:, 0:1])
-        for c in range(CHUNKS):
-            quantise_weight_chunk(w2_chunks[c], w2_codes[:, c, :], w2_scales[:, c, :])
+        def add_slopes(r):
+            slopes = psum.tile([P, N_HALF], F32, tag="back", bufs=ROW_BLOCKS)
+            nc.tensor.matmul(out=slopes[:], lhsT=ident_bf16[:], rhs=k1_sb[:, r, left], start=True, stop=False)
+            nc.tensor.matmul(out=slopes[:], lhsT=twice_ident[:], rhs=k2_sb[:, r, left], start=False, stop=False)
+            nc.tensor.matmul(out=slopes[:], lhsT=twice_ident[:], rhs=k3_sb[:, r, left], start=False, stop=True)
+            slope_sums.append(slopes)
+            nc.vector.tensor_tensor(out=base[:, r, right], in0=k2_sb[:, r, right], in1=k3_sb[:, r, right], op=ALU.add)
             nc.vector.scalar_tensor_tensor(
-                out=base[:, c, :],
-                in0=base[:, c, :],
-                scalar=dt_sixth[:, 0:1],
-                in1=h_sb[:, c, :],
+                out=base[:, r, right],
+                in0=base[:, r, right],
+                scalar=2.0,
+                in1=k1_sb[:, r, right],
                 op0=ALU.mult,
                 op1=ALU.add,
             )
 
-        tiles_per_half = N_HALF // P
+        def finish_base(r):
+            nc.vector.scalar_tensor_tensor(
+                out=base[:, r, left],
+                in0=slope_sums[r][:],
+                scalar=dt_sixth[:, 0:1],
+                in1=h_sb[:, r, left],
+                op0=ALU.mult,
+                op1=ALU.add,
+            )
+            nc.vector.scalar_tensor_tensor(
+                out=base[:, r, right],
+                in0=base[:, r, right],
+                scalar=dt_sixth[:, 0:1],
+                in1=h_sb[:, r, right],
+                op0=ALU.mult,
+                op1=ALU.add,
+            )
+
+        for i in range(2 * CHUNKS + QUANTISE_LAG):
+            if i < 2 * CHUNKS:
+                transpose_chunk(i)
+            if i >= QUANTISE_LAG:
+                quantise_chunk(i - QUANTISE_LAG)
+            if 0 <= i - LAYER_LAG < CHUNKS:
+                first_layer(i - LAYER_LAG)
+            if i < ROW_BLOCKS:
+                add_slopes(i)
+            for g in range(PASSES):
+                if i - Z_LAG == 2 * g + 1:
+                    quantise_z(g)
+            if 0 <= i - ROW_BLOCKS < ROW_BLOCKS:
+                finish_base(i - ROW_BLOCKS)
+        nc.vector.tensor_scalar_mul(out=b2_scaled[:], in0=b2_cols[:], scalar1=dt_sixth[:, 0:1])
+
+        k4_tiles = []
         for half in range(HALVES):
-            k4_t = stage.tile([P, tiles_per_half, B], F32)
-            for s in range(tiles_per_half):
-                tile_index = half * tiles_per_half + s
-                c = tile_index // BLOCKS_PER_CHUNK
-                e = tile_index % BLOCKS_PER_CHUNK
-                acc = psum.tile([P, B], F32, tag="acc")
-                for g in range(PASSES):
-                    cols = slice(g * CHUNK_ROWS + e * P, g * CHUNK_ROWS + (e + 1) * P)
-                    nc.tensor.matmul_mx(
-                        out=acc[:],
-                        lhsT=w2_codes[:, c, cols].bitcast(FP8X4),
-                        lhsT_scale=w2_scales[:, c, cols],
-                        rhs=z_codes[:, g, :].bitcast(FP8X4),
-                        rhs_scale=z_scales[:, g, :],
-                        start=(g == 0),
-                        stop=(g == PASSES - 1),
-                    )
+            k4_t = stage.tile([P, TILES_PER_HALF, B], F32, bufs=HALVES)
+            k4_tiles.append(k4_t)
+            for s in range(TILES_PER_HALF):
+                tile_index = half * TILES_PER_HALF + s
+                acc = weights_times(
+                    CHUNKS + tile_index // TILES_PER_CHUNK, tile_index % TILES_PER_CHUNK, z_codes, z_scales
+                )
                 nc.scalar.activation(
                     out=k4_t[:, s, :],
                     in_=acc[:],
@@ -248,14 +281,15 @@ def tile_nodelstmcell_pc_kernel(tc, h_tilde, k1, k2, k3, t0, t1, W1, b1, W2, b2,
                     bias=b2_scaled[:, tile_index : tile_index + 1],
                     scale=dt_sixth[:, 0:1],
                 )
+        for half in range(HALVES):
+            cols = slice(half * N_HALF, (half + 1) * N_HALF)
             for r in range(ROW_BLOCKS):
                 back = psum.tile([P, N_HALF], F32, tag="back", bufs=ROW_BLOCKS)
-                for s in range(tiles_per_half):
+                for s in range(TILES_PER_HALF):
                     nc.tensor.transpose(
                         out=back[:, s * P : (s + 1) * P],
-                        in_=k4_t[:, s, r * P : (r + 1) * P],
+                        in_=k4_tiles[half][:, s, r * P : (r + 1) * P],
                         identity=ident_f32[:],
                     )
-                cols = slice(half * N_HALF, (half + 1) * N_HALF)
                 nc.vector.tensor_tensor(out=base[:, r, cols], in0=back[:], in1=base[:, r, cols], op=ALU.add)
                 nc.sync.dma_start(out=out_rows[:, r, cols], in_=base[:, r, cols])

@@ -22,6 +22,7 @@ CHUNKS = 4
 CHUNK_ROWS = H // CHUNKS
 TILES_PER_CHUNK = CHUNK_ROWS // P
 WORDS = H // 2
+W1_PITCH = H + 16
 N_HALF = 512
 HALVES = H // N_HALF
 TILES_PER_HALF = N_HALF // P
@@ -37,13 +38,12 @@ def tile_nodelstmcell_pc_kernel(tc, h_tilde, k1, k2, k3, t0, t1, W1, b1, W2, b2,
     left = slice(0, N_HALF)
     right = slice(N_HALF, H)
     with ExitStack() as ctx:
-        ctx.enter_context(tc.manual_schedule())
         const = ctx.enter_context(tc.tile_pool(name="const", bufs=1))
         data = ctx.enter_context(tc.tile_pool(name="data", bufs=1))
         weights = ctx.enter_context(tc.tile_pool(name="weights", bufs=CHUNKS))
         stage = ctx.enter_context(tc.tile_pool(name="stage", bufs=3))
         keep = ctx.enter_context(tc.tile_pool(name="keep", bufs=1))
-        psum = ctx.enter_context(tc.psum_pool(name="psum", bufs=2))
+        psum = ctx.enter_context(tc.psum_pool(name="psum", bufs=3))
 
         t0_all = const.tile([P, 1], BF16)
         t1_all = const.tile([P, 1], BF16)
@@ -71,7 +71,7 @@ def tile_nodelstmcell_pc_kernel(tc, h_tilde, k1, k2, k3, t0, t1, W1, b1, W2, b2,
             nc.sync.dma_start(out=b1_cols[:], in_=b1.rearrange("(c p e) -> p c e", p=P, e=TILES_PER_CHUNK))
         chunk_tiles = []
         for c in range(CHUNKS):
-            w1_c = weights.tile([P, TILES_PER_CHUNK, H + 2], BF16)
+            w1_c = weights.tile([P, TILES_PER_CHUNK, W1_PITCH], BF16)
             nc.sync.dma_start(out=w1_c[:, :, 0 : H + 1], in_=w1_view[c])
             chunk_tiles.append(w1_c)
             nc.sync.dma_start(out=k2_sb[:, c, :], in_=k2_rows[:, c, :])
@@ -216,7 +216,7 @@ def tile_nodelstmcell_pc_kernel(tc, h_tilde, k1, k2, k3, t0, t1, W1, b1, W2, b2,
             )
 
         def add_slopes(r):
-            slopes = psum.tile([P, N_HALF], F32, tag="back", bufs=ROW_BLOCKS)
+            slopes = psum.tile([P, N_HALF], F32, tag="sum", bufs=2)
             nc.tensor.matmul(out=slopes[:], lhsT=ident_bf16[:], rhs=k1_sb[:, r, left], start=True, stop=False)
             nc.tensor.matmul(out=slopes[:], lhsT=twice_ident[:], rhs=k2_sb[:, r, left], start=False, stop=False)
             nc.tensor.matmul(out=slopes[:], lhsT=twice_ident[:], rhs=k3_sb[:, r, left], start=False, stop=True)
@@ -231,20 +231,12 @@ def tile_nodelstmcell_pc_kernel(tc, h_tilde, k1, k2, k3, t0, t1, W1, b1, W2, b2,
                 op1=ALU.add,
             )
 
-        def finish_base(r):
+        def finish_base(r, cols, slopes):
             nc.vector.scalar_tensor_tensor(
-                out=base[:, r, left],
-                in0=slope_sums[r][:],
+                out=base[:, r, cols],
+                in0=slopes,
                 scalar=dt_sixth[:, 0:1],
-                in1=h_sb[:, r, left],
-                op0=ALU.mult,
-                op1=ALU.add,
-            )
-            nc.vector.scalar_tensor_tensor(
-                out=base[:, r, right],
-                in0=base[:, r, right],
-                scalar=dt_sixth[:, 0:1],
-                in1=h_sb[:, r, right],
+                in1=h_sb[:, r, cols],
                 op0=ALU.mult,
                 op1=ALU.add,
             )
@@ -258,11 +250,13 @@ def tile_nodelstmcell_pc_kernel(tc, h_tilde, k1, k2, k3, t0, t1, W1, b1, W2, b2,
                 first_layer(i - LAYER_LAG)
             if i < ROW_BLOCKS:
                 add_slopes(i)
+            if 0 <= i - 1 < ROW_BLOCKS:
+                finish_base(i - 1, left, slope_sums[i - 1][:])
             for g in range(PASSES):
                 if i - Z_LAG == 2 * g + 1:
                     quantise_z(g)
             if 0 <= i - ROW_BLOCKS < ROW_BLOCKS:
-                finish_base(i - ROW_BLOCKS)
+                finish_base(i - ROW_BLOCKS, right, base[:, i - ROW_BLOCKS, right])
         nc.vector.tensor_scalar_mul(out=b2_scaled[:], in0=b2_cols[:], scalar1=dt_sixth[:, 0:1])
 
         k4_tiles = []
@@ -284,7 +278,7 @@ def tile_nodelstmcell_pc_kernel(tc, h_tilde, k1, k2, k3, t0, t1, W1, b1, W2, b2,
         for half in range(HALVES):
             cols = slice(half * N_HALF, (half + 1) * N_HALF)
             for r in range(ROW_BLOCKS):
-                back = psum.tile([P, N_HALF], F32, tag="back", bufs=ROW_BLOCKS)
+                back = psum.tile([P, N_HALF], F32, tag="tp")
                 for s in range(TILES_PER_HALF):
                     nc.tensor.transpose(
                         out=back[:, s * P : (s + 1) * P],

@@ -43,7 +43,7 @@ def tile_nodelstmcell_pc_kernel(tc, h_tilde, k1, k2, k3, t0, t1, W1, b1, W2, b2,
         weights = ctx.enter_context(tc.tile_pool(name="weights", bufs=CHUNKS))
         stage = ctx.enter_context(tc.tile_pool(name="stage", bufs=3))
         keep = ctx.enter_context(tc.tile_pool(name="keep", bufs=1))
-        psum = ctx.enter_context(tc.psum_pool(name="psum", bufs=3))
+        psum = ctx.enter_context(tc.psum_pool(name="psum", bufs=4))
 
         t0_all = const.tile([P, 1], BF16)
         t1_all = const.tile([P, 1], BF16)
@@ -144,7 +144,6 @@ def tile_nodelstmcell_pc_kernel(tc, h_tilde, k1, k2, k3, t0, t1, W1, b1, W2, b2,
         z_scales = keep.tile([P, PASSES, B], U8, align_bytes=64)
         base = keep.tile([P, ROW_BLOCKS, H], F32)
         grouped_tiles = []
-        slope_sums = []
 
         def transpose_chunk(i):
             w_words = chunk_tiles[i][:].bitcast(F32)
@@ -216,11 +215,6 @@ def tile_nodelstmcell_pc_kernel(tc, h_tilde, k1, k2, k3, t0, t1, W1, b1, W2, b2,
             )
 
         def add_slopes(r):
-            slopes = psum.tile([P, N_HALF], F32, tag="sum", bufs=2)
-            nc.tensor.matmul(out=slopes[:], lhsT=ident_bf16[:], rhs=k1_sb[:, r, left], start=True, stop=False)
-            nc.tensor.matmul(out=slopes[:], lhsT=twice_ident[:], rhs=k2_sb[:, r, left], start=False, stop=False)
-            nc.tensor.matmul(out=slopes[:], lhsT=twice_ident[:], rhs=k3_sb[:, r, left], start=False, stop=True)
-            slope_sums.append(slopes)
             nc.vector.tensor_tensor(out=base[:, r, right], in0=k2_sb[:, r, right], in1=k3_sb[:, r, right], op=ALU.add)
             nc.vector.scalar_tensor_tensor(
                 out=base[:, r, right],
@@ -231,10 +225,10 @@ def tile_nodelstmcell_pc_kernel(tc, h_tilde, k1, k2, k3, t0, t1, W1, b1, W2, b2,
                 op1=ALU.add,
             )
 
-        def finish_base(r, cols, slopes):
+        def scale_and_add_h(r, cols, total):
             nc.vector.scalar_tensor_tensor(
                 out=base[:, r, cols],
-                in0=slopes,
+                in0=total,
                 scalar=dt_sixth[:, 0:1],
                 in1=h_sb[:, r, cols],
                 op0=ALU.mult,
@@ -250,13 +244,11 @@ def tile_nodelstmcell_pc_kernel(tc, h_tilde, k1, k2, k3, t0, t1, W1, b1, W2, b2,
                 first_layer(i - LAYER_LAG)
             if i < ROW_BLOCKS:
                 add_slopes(i)
-            if 0 <= i - 1 < ROW_BLOCKS:
-                finish_base(i - 1, left, slope_sums[i - 1][:])
             for g in range(PASSES):
                 if i - Z_LAG == 2 * g + 1:
                     quantise_z(g)
             if 0 <= i - ROW_BLOCKS < ROW_BLOCKS:
-                finish_base(i - ROW_BLOCKS, right, base[:, i - ROW_BLOCKS, right])
+                scale_and_add_h(i - ROW_BLOCKS, right, base[:, i - ROW_BLOCKS, right])
         nc.vector.tensor_scalar_mul(out=b2_scaled[:], in0=b2_cols[:], scalar1=dt_sixth[:, 0:1])
 
         k4_tiles = []
@@ -268,22 +260,45 @@ def tile_nodelstmcell_pc_kernel(tc, h_tilde, k1, k2, k3, t0, t1, W1, b1, W2, b2,
                 acc = weights_times(
                     CHUNKS + tile_index // TILES_PER_CHUNK, tile_index % TILES_PER_CHUNK, z_codes, z_scales
                 )
-                nc.scalar.activation(
-                    out=k4_t[:, s, :],
-                    in_=acc[:],
-                    func=ACT.Identity,
-                    bias=b2_scaled[:, tile_index : tile_index + 1],
-                    scale=dt_sixth[:, 0:1],
-                )
-        for half in range(HALVES):
-            cols = slice(half * N_HALF, (half + 1) * N_HALF)
-            for r in range(ROW_BLOCKS):
-                back = psum.tile([P, N_HALF], F32, tag="tp")
-                for s in range(TILES_PER_HALF):
-                    nc.tensor.transpose(
-                        out=back[:, s * P : (s + 1) * P],
-                        in_=k4_tiles[half][:, s, r * P : (r + 1) * P],
-                        identity=ident_f32[:],
+                if half == 0:
+                    nc.scalar.activation(
+                        out=k4_t[:, s, :],
+                        in_=acc[:],
+                        func=ACT.Identity,
+                        bias=b2_cols[:, tile_index : tile_index + 1],
+                        scale=1.0,
                     )
-                nc.vector.tensor_tensor(out=base[:, r, cols], in0=back[:], in1=base[:, r, cols], op=ALU.add)
-                nc.sync.dma_start(out=out_rows[:, r, cols], in_=base[:, r, cols])
+                else:
+                    nc.scalar.activation(
+                        out=k4_t[:, s, :],
+                        in_=acc[:],
+                        func=ACT.Identity,
+                        bias=b2_scaled[:, tile_index : tile_index + 1],
+                        scale=dt_sixth[:, 0:1],
+                    )
+        for r in range(ROW_BLOCKS):
+            total = psum.tile([P, N_HALF], F32, tag="tp")
+            nc.tensor.matmul(out=total[:], lhsT=ident_bf16[:], rhs=k1_sb[:, r, left], start=True, stop=False)
+            nc.tensor.matmul(out=total[:], lhsT=twice_ident[:], rhs=k2_sb[:, r, left], start=False, stop=False)
+            nc.tensor.matmul(out=total[:], lhsT=twice_ident[:], rhs=k3_sb[:, r, left], start=False, stop=False)
+            for s in range(TILES_PER_HALF):
+                nc.tensor.matmul(
+                    out=total[:, s * P : (s + 1) * P],
+                    lhsT=k4_tiles[0][:, s, r * P : (r + 1) * P],
+                    rhs=ident_f32[:],
+                    is_transpose=True,
+                    start=False,
+                    stop=(s == TILES_PER_HALF - 1),
+                )
+            scale_and_add_h(r, left, total[:])
+            nc.sync.dma_start(out=out_rows[:, r, left], in_=base[:, r, left])
+        for r in range(ROW_BLOCKS):
+            back = psum.tile([P, N_HALF], F32, tag="tp")
+            for s in range(TILES_PER_HALF):
+                nc.tensor.transpose(
+                    out=back[:, s * P : (s + 1) * P],
+                    in_=k4_tiles[1][:, s, r * P : (r + 1) * P],
+                    identity=ident_f32[:],
+                )
+            nc.vector.tensor_tensor(out=base[:, r, right], in0=back[:], in1=base[:, r, right], op=ALU.add)
+            nc.sync.dma_start(out=out_rows[:, r, right], in_=base[:, r, right])

@@ -25,7 +25,6 @@ WORDS = H // 2
 W1_PITCH = H + 16
 N_HALF = 512
 HALVES = H // N_HALF
-TILES_PER_HALF = N_HALF // P
 QUANTISE_LAG = 1
 LAYER_LAG = 2
 Z_LAG = 3
@@ -43,7 +42,7 @@ def tile_nodelstmcell_pc_kernel(tc, h_tilde, k1, k2, k3, t0, t1, W1, b1, W2, b2,
         weights = ctx.enter_context(tc.tile_pool(name="weights", bufs=CHUNKS))
         stage = ctx.enter_context(tc.tile_pool(name="stage", bufs=3))
         keep = ctx.enter_context(tc.tile_pool(name="keep", bufs=1))
-        psum = ctx.enter_context(tc.psum_pool(name="psum", bufs=4))
+        psum = ctx.enter_context(tc.psum_pool(name="psum", bufs=3))
 
         t0_all = const.tile([P, 1], BF16)
         t1_all = const.tile([P, 1], BF16)
@@ -67,8 +66,9 @@ def tile_nodelstmcell_pc_kernel(tc, h_tilde, k1, k2, k3, t0, t1, W1, b1, W2, b2,
         for r in range(ROW_BLOCKS):
             nc.sync.dma_start(out=h_sb[:, r, :], in_=h_rows[:, r, :])
             nc.sync.dma_start(out=k3_sb[:, r, :], in_=k3_rows[:, r, :])
-        with nc.allow_non_contiguous_dma(reason="a bias vector of 2 KiB, two values to a partition"):
+        with nc.allow_non_contiguous_dma(reason="two bias vectors of 2 KiB, two values or one to a partition"):
             nc.sync.dma_start(out=b1_cols[:], in_=b1.rearrange("(c p e) -> p c e", p=P, e=TILES_PER_CHUNK))
+            nc.sync.dma_start(out=b2_cols[:], in_=b2.rearrange("(s p) -> p s", p=P))
         chunk_tiles = []
         for c in range(CHUNKS):
             w1_c = weights.tile([P, TILES_PER_CHUNK, W1_PITCH], BF16)
@@ -80,8 +80,6 @@ def tile_nodelstmcell_pc_kernel(tc, h_tilde, k1, k2, k3, t0, t1, W1, b1, W2, b2,
             w2_c = weights.tile([P, TILES_PER_CHUNK, H], BF16)
             nc.sync.dma_start(out=w2_c[:], in_=w2_view[c])
             chunk_tiles.append(w2_c)
-        with nc.allow_non_contiguous_dma(reason="a bias vector of 2 KiB, one value to a partition"):
-            nc.sync.dma_start(out=b2_cols[:], in_=b2.rearrange("(s p) -> p s", p=P))
 
         ident_f32 = const.tile([P, P], F32)
         make_identity(nc, ident_f32[:])
@@ -134,16 +132,17 @@ def tile_nodelstmcell_pc_kernel(tc, h_tilde, k1, k2, k3, t0, t1, W1, b1, W2, b2,
             in_=y_grouped[:].rearrange("p g b t -> p (g b t)"),
         )
 
-        w_codes = keep.tile([P, 2 * CHUNKS, PASSES * CHUNK_ROWS], U32, align_bytes=64)
-        w_scales = keep.tile([P, 2 * CHUNKS, PASSES * CHUNK_ROWS], U8, align_bytes=64)
+        w_codes = keep.tile([P, 2, PASSES, H], U32, align_bytes=64)
+        w_scales = keep.tile([P, 2, PASSES, H], U8, align_bytes=64)
         bias1 = const.tile([P, CHUNKS, TILES_PER_CHUNK], F32)
-        b2_scaled = const.tile([P, H // P], F32)
+        b2_all = const.tile([P, H], BF16)
         z_sb = keep.tile([P, H // P, B], BF16)
         z_grouped = keep.tile([P, PASSES, B * PACK], BF16, align_bytes=64)
         z_codes = keep.tile([P, PASSES, B], U32, align_bytes=64)
         z_scales = keep.tile([P, PASSES, B], U8, align_bytes=64)
         base = keep.tile([P, ROW_BLOCKS, H], F32)
         grouped_tiles = []
+        slope_sums = []
 
         def transpose_chunk(i):
             w_words = chunk_tiles[i][:].bitcast(F32)
@@ -165,20 +164,21 @@ def tile_nodelstmcell_pc_kernel(tc, h_tilde, k1, k2, k3, t0, t1, W1, b1, W2, b2,
             grouped_tiles.append(grouped)
 
         def quantise_chunk(i):
-            nc.vector.quantize_mx(
-                out=w_codes[:, i, :].bitcast(FP8X4),
-                scales=w_scales[:, i, :],
-                in_=grouped_tiles[i][:].rearrange("p g x -> p (g x)"),
-            )
-
-        def weights_times(i, s, moving_codes, moving_scales):
-            acc = psum.tile([P, B], F32, tag="acc")
+            rows = slice((i % CHUNKS) * CHUNK_ROWS, (i % CHUNKS + 1) * CHUNK_ROWS)
             for g in range(PASSES):
-                cols = slice(g * CHUNK_ROWS + s * P, g * CHUNK_ROWS + (s + 1) * P)
+                nc.vector.quantize_mx(
+                    out=w_codes[:, i // CHUNKS, g, rows].bitcast(FP8X4),
+                    scales=w_scales[:, i // CHUNKS, g, rows],
+                    in_=grouped_tiles[i][:, g, :],
+                )
+
+        def multiply(still_codes, still_scales, moving_codes, moving_scales):
+            acc = psum.tile([P, N_HALF], F32, tag="acc")
+            for g in range(PASSES):
                 nc.tensor.matmul_mx(
                     out=acc[:],
-                    lhsT=w_codes[:, i, cols].bitcast(FP8X4),
-                    lhsT_scale=w_scales[:, i, cols],
+                    lhsT=still_codes[:, g, :].bitcast(FP8X4),
+                    lhsT_scale=still_scales[:, g, :],
                     rhs=moving_codes[:, g, :].bitcast(FP8X4),
                     rhs_scale=moving_scales[:, g, :],
                     start=(g == 0),
@@ -196,7 +196,8 @@ def tile_nodelstmcell_pc_kernel(tc, h_tilde, k1, k2, k3, t0, t1, W1, b1, W2, b2,
                 op1=ALU.add,
             )
             for e in range(TILES_PER_CHUNK):
-                acc = weights_times(c, e, y_codes, y_scales)
+                rows = slice((TILES_PER_CHUNK * c + e) * P, (TILES_PER_CHUNK * c + e + 1) * P)
+                acc = multiply(w_codes[:, 0, :, rows], w_scales[:, 0, :, rows], y_codes, y_scales)
                 nc.scalar.activation(
                     out=z_sb[:, TILES_PER_CHUNK * c + e, :],
                     in_=acc[:],
@@ -206,7 +207,7 @@ def tile_nodelstmcell_pc_kernel(tc, h_tilde, k1, k2, k3, t0, t1, W1, b1, W2, b2,
                 )
 
         def quantise_z(g):
-            nc.vector.tensor_copy(
+            nc.scalar.copy(
                 out=z_grouped[:, g, :].rearrange("p (c i t) -> p c t i", i=4, t=PACK),
                 in_=z_sb[:, PACK * g : PACK * (g + 1), :].rearrange("p t (c i) -> p c t i", i=4),
             )
@@ -215,6 +216,11 @@ def tile_nodelstmcell_pc_kernel(tc, h_tilde, k1, k2, k3, t0, t1, W1, b1, W2, b2,
             )
 
         def add_slopes(r):
+            slopes = psum.tile([P, N_HALF], F32, tag="sum", bufs=2)
+            nc.tensor.matmul(out=slopes[:], lhsT=ident_bf16[:], rhs=k1_sb[:, r, left], start=True, stop=False)
+            nc.tensor.matmul(out=slopes[:], lhsT=twice_ident[:], rhs=k2_sb[:, r, left], start=False, stop=False)
+            nc.tensor.matmul(out=slopes[:], lhsT=twice_ident[:], rhs=k3_sb[:, r, left], start=False, stop=True)
+            slope_sums.append(slopes)
             nc.vector.tensor_tensor(out=base[:, r, right], in0=k2_sb[:, r, right], in1=k3_sb[:, r, right], op=ALU.add)
             nc.vector.scalar_tensor_tensor(
                 out=base[:, r, right],
@@ -225,15 +231,25 @@ def tile_nodelstmcell_pc_kernel(tc, h_tilde, k1, k2, k3, t0, t1, W1, b1, W2, b2,
                 op1=ALU.add,
             )
 
-        def scale_and_add_h(r, cols, total):
+        def finish_base(r, cols, slopes):
+            nc.vector.tensor_tensor(out=base[:, r, cols], in0=slopes, in1=b2_all[:, cols], op=ALU.add)
             nc.vector.scalar_tensor_tensor(
                 out=base[:, r, cols],
-                in0=total,
+                in0=base[:, r, cols],
                 scalar=dt_sixth[:, 0:1],
                 in1=h_sb[:, r, cols],
                 op0=ALU.mult,
                 op1=ALU.add,
             )
+
+        b2_t = psum.tile([P, H], BF16, tag="tp")
+        for s in range(H // P):
+            nc.tensor.transpose(
+                out=b2_t[:, s * P : (s + 1) * P],
+                in_=b2_cols[:, s : s + 1].to_broadcast([P, P]),
+                identity=ident_bf16[:],
+            )
+        nc.scalar.copy(out=b2_all[:], in_=b2_t[:])
 
         for i in range(2 * CHUNKS + QUANTISE_LAG):
             if i < 2 * CHUNKS:
@@ -244,61 +260,27 @@ def tile_nodelstmcell_pc_kernel(tc, h_tilde, k1, k2, k3, t0, t1, W1, b1, W2, b2,
                 first_layer(i - LAYER_LAG)
             if i < ROW_BLOCKS:
                 add_slopes(i)
+            if 0 <= i - 1 < ROW_BLOCKS:
+                finish_base(i - 1, left, slope_sums[i - 1][:])
             for g in range(PASSES):
                 if i - Z_LAG == 2 * g + 1:
                     quantise_z(g)
             if 0 <= i - ROW_BLOCKS < ROW_BLOCKS:
-                scale_and_add_h(i - ROW_BLOCKS, right, base[:, i - ROW_BLOCKS, right])
-        nc.vector.tensor_scalar_mul(out=b2_scaled[:], in0=b2_cols[:], scalar1=dt_sixth[:, 0:1])
+                finish_base(i - ROW_BLOCKS, right, base[:, i - ROW_BLOCKS, right])
 
-        k4_tiles = []
         for half in range(HALVES):
-            k4_t = stage.tile([P, TILES_PER_HALF, B], F32, bufs=HALVES)
-            k4_tiles.append(k4_t)
-            for s in range(TILES_PER_HALF):
-                tile_index = half * TILES_PER_HALF + s
-                acc = weights_times(
-                    CHUNKS + tile_index // TILES_PER_CHUNK, tile_index % TILES_PER_CHUNK, z_codes, z_scales
+            cols = slice(half * N_HALF, (half + 1) * N_HALF)
+            for r in range(ROW_BLOCKS):
+                batch = slice(r * P, (r + 1) * P)
+                acc = multiply(
+                    z_codes[:, :, batch], z_scales[:, :, batch], w_codes[:, 1, :, cols], w_scales[:, 1, :, cols]
                 )
-                if half == 0:
-                    nc.scalar.activation(
-                        out=k4_t[:, s, :],
-                        in_=acc[:],
-                        func=ACT.Identity,
-                        bias=b2_cols[:, tile_index : tile_index + 1],
-                        scale=1.0,
-                    )
-                else:
-                    nc.scalar.activation(
-                        out=k4_t[:, s, :],
-                        in_=acc[:],
-                        func=ACT.Identity,
-                        bias=b2_scaled[:, tile_index : tile_index + 1],
-                        scale=dt_sixth[:, 0:1],
-                    )
-        for r in range(ROW_BLOCKS):
-            total = psum.tile([P, N_HALF], F32, tag="tp")
-            nc.tensor.matmul(out=total[:], lhsT=ident_bf16[:], rhs=k1_sb[:, r, left], start=True, stop=False)
-            nc.tensor.matmul(out=total[:], lhsT=twice_ident[:], rhs=k2_sb[:, r, left], start=False, stop=False)
-            nc.tensor.matmul(out=total[:], lhsT=twice_ident[:], rhs=k3_sb[:, r, left], start=False, stop=False)
-            for s in range(TILES_PER_HALF):
-                nc.tensor.matmul(
-                    out=total[:, s * P : (s + 1) * P],
-                    lhsT=k4_tiles[0][:, s, r * P : (r + 1) * P],
-                    rhs=ident_f32[:],
-                    is_transpose=True,
-                    start=False,
-                    stop=(s == TILES_PER_HALF - 1),
+                nc.vector.scalar_tensor_tensor(
+                    out=base[:, r, cols],
+                    in0=acc[:],
+                    scalar=dt_sixth[:, 0:1],
+                    in1=base[:, r, cols],
+                    op0=ALU.mult,
+                    op1=ALU.add,
                 )
-            scale_and_add_h(r, left, total[:])
-            nc.sync.dma_start(out=out_rows[:, r, left], in_=base[:, r, left])
-        for r in range(ROW_BLOCKS):
-            back = psum.tile([P, N_HALF], F32, tag="tp")
-            for s in range(TILES_PER_HALF):
-                nc.tensor.transpose(
-                    out=back[:, s * P : (s + 1) * P],
-                    in_=k4_tiles[1][:, s, r * P : (r + 1) * P],
-                    identity=ident_f32[:],
-                )
-            nc.vector.tensor_tensor(out=base[:, r, right], in0=back[:], in1=base[:, r, right], op=ALU.add)
-            nc.sync.dma_start(out=out_rows[:, r, right], in_=base[:, r, right])
+                nc.sync.dma_start(out=out_rows[:, r, cols], in_=base[:, r, cols])

@@ -36,6 +36,10 @@ def tile_nodelstmcell_pc_kernel(tc, h_tilde, k1, k2, k3, t0, t1, W1, b1, W2, b2,
     nc = tc.nc
     left = slice(0, N_HALF)
     right = slice(N_HALF, H)
+
+    def y_parts(r):
+        return (left, right) if r == 0 else (slice(0, H),)
+
     with ExitStack() as ctx:
         const = ctx.enter_context(tc.tile_pool(name="const", bufs=1))
         data = ctx.enter_context(tc.tile_pool(name="data", bufs=1))
@@ -64,8 +68,9 @@ def tile_nodelstmcell_pc_kernel(tc, h_tilde, k1, k2, k3, t0, t1, W1, b1, W2, b2,
         w2_view = W2.rearrange("(c s p) k -> c p s k", s=TILES_PER_CHUNK, p=P)
 
         for r in range(ROW_BLOCKS):
-            nc.sync.dma_start(out=h_sb[:, r, :], in_=h_rows[:, r, :])
-            nc.sync.dma_start(out=k3_sb[:, r, :], in_=k3_rows[:, r, :])
+            for cols in y_parts(r):
+                nc.sync.dma_start(out=h_sb[:, r, cols], in_=h_rows[:, r, cols])
+                nc.sync.dma_start(out=k3_sb[:, r, cols], in_=k3_rows[:, r, cols])
         with nc.allow_non_contiguous_dma(reason="two bias vectors of 2 KiB, two values or one to a partition"):
             nc.sync.dma_start(out=b1_cols[:], in_=b1.rearrange("(c p e) -> p c e", p=P, e=TILES_PER_CHUNK))
             nc.sync.dma_start(out=b2_cols[:], in_=b2.rearrange("(s p) -> p s", p=P))
@@ -99,32 +104,36 @@ def tile_nodelstmcell_pc_kernel(tc, h_tilde, k1, k2, k3, t0, t1, W1, b1, W2, b2,
         nc.vector.tensor_tensor(out=t_end[:], in0=t0_all[:], in1=dt[:], op=ALU.add)
         nc.vector.tensor_scalar_mul(out=dt_sixth[:], in0=dt[:], scalar1=1.0 / 6.0)
 
-        y_split = keep.tile([P, ROW_BLOCKS, 2, WORDS], BF16)
+        y_sb = keep.tile([P, ROW_BLOCKS, H], BF16)
         y_grouped = keep.tile([P, PASSES, B, PACK], BF16, align_bytes=64)
         y_codes = keep.tile([P, PASSES, B], U32, align_bytes=64)
         y_scales = keep.tile([P, PASSES, B], U8, align_bytes=64)
         for r in range(ROW_BLOCKS):
-            nc.vector.scalar_tensor_tensor(
-                out=y_split[:, r, :, :],
-                in0=k3_sb[:, r, :].rearrange("p (w e) -> p e w", e=2),
-                scalar=dt[:, 0:1],
-                in1=h_sb[:, r, :].rearrange("p (w e) -> p e w", e=2),
-                op0=ALU.mult,
-                op1=ALU.add,
-            )
-            y_t = psum.tile([P, PASSES, PACK, P], BF16, tag="tp")
+            for cols in y_parts(r):
+                nc.vector.scalar_tensor_tensor(
+                    out=y_sb[:, r, cols],
+                    in0=k3_sb[:, r, cols],
+                    scalar=dt[:, 0:1],
+                    in1=h_sb[:, r, cols],
+                    op0=ALU.mult,
+                    op1=ALU.add,
+                )
+            y_words = y_sb[:, r, :].bitcast(F32)
+            y_t = psum.tile([P, PASSES, 2, P], F32, tag="tp")
             for g in range(PASSES):
                 for u in range(2):
-                    for e in range(2):
-                        first = (2 * g + u) * P
-                        nc.tensor.transpose(
-                            out=y_t[:, g, 2 * u + e, :],
-                            in_=y_split[:, r, e, first : first + P],
-                            identity=ident_bf16[:],
-                        )
+                    first = (2 * g + u) * P
+                    nc.tensor.transpose(
+                        out=y_t[:, g, u, :],
+                        in_=y_words[:, first : first + P],
+                        identity=ident_f32[:],
+                    )
             nc.scalar.copy(
-                out=y_grouped[:, :, r * P : (r + 1) * P, :],
-                in_=y_t[:].rearrange("p g t b -> p g b t"),
+                out=y_grouped[:, :, r * P : (r + 1) * P, :]
+                .rearrange("p g b t -> p g (b t)")
+                .bitcast(F32)
+                .rearrange("p g (b u) -> p g b u", u=2),
+                in_=y_t[:].rearrange("p g u b -> p g b u"),
             )
         nc.vector.quantize_mx(
             out=y_codes[:].rearrange("p g b -> p (g b)").bitcast(FP8X4),
@@ -187,14 +196,10 @@ def tile_nodelstmcell_pc_kernel(tc, h_tilde, k1, k2, k3, t0, t1, W1, b1, W2, b2,
             return acc
 
         def first_layer(c):
-            nc.vector.scalar_tensor_tensor(
-                out=bias1[:, c, :],
-                in0=chunk_tiles[c][:, :, H],
-                scalar=t_end[:, 0:1],
-                in1=b1_cols[:, c, :],
-                op0=ALU.mult,
-                op1=ALU.add,
+            nc.gpsimd.tensor_scalar(
+                out=bias1[:, c, :], in0=chunk_tiles[c][:, :, H], scalar1=t_end[:, 0:1], scalar2=None, op0=ALU.mult
             )
+            nc.gpsimd.tensor_tensor(out=bias1[:, c, :], in0=bias1[:, c, :], in1=b1_cols[:, c, :], op=ALU.add)
             for e in range(TILES_PER_CHUNK):
                 rows = slice((TILES_PER_CHUNK * c + e) * P, (TILES_PER_CHUNK * c + e + 1) * P)
                 acc = multiply(w_codes[:, 0, :, rows], w_scales[:, 0, :, rows], y_codes, y_scales)
@@ -275,12 +280,17 @@ def tile_nodelstmcell_pc_kernel(tc, h_tilde, k1, k2, k3, t0, t1, W1, b1, W2, b2,
                 acc = multiply(
                     z_codes[:, :, batch], z_scales[:, :, batch], w_codes[:, 1, :, cols], w_scales[:, 1, :, cols]
                 )
-                nc.vector.scalar_tensor_tensor(
-                    out=base[:, r, cols],
-                    in0=acc[:],
-                    scalar=dt_sixth[:, 0:1],
-                    in1=base[:, r, cols],
-                    op0=ALU.mult,
-                    op1=ALU.add,
-                )
-                nc.sync.dma_start(out=out_rows[:, r, cols], in_=base[:, r, cols])
+                parts = 2 if half == HALVES - 1 and r == ROW_BLOCKS - 1 else 1
+                width = N_HALF // parts
+                for part in range(parts):
+                    inner = slice(part * width, (part + 1) * width)
+                    outer = slice(half * N_HALF + part * width, half * N_HALF + (part + 1) * width)
+                    nc.vector.scalar_tensor_tensor(
+                        out=base[:, r, outer],
+                        in0=acc[:, inner],
+                        scalar=dt_sixth[:, 0:1],
+                        in1=base[:, r, outer],
+                        op0=ALU.mult,
+                        op1=ALU.add,
+                    )
+                    nc.sync.dma_start(out=out_rows[:, r, outer], in_=base[:, r, outer])

@@ -67,24 +67,49 @@ def tile_nodelstmcell_pc_kernel(tc, h_tilde, k1, k2, k3, t0, t1, W1, b1, W2, b2,
         w1_view = W1.rearrange("(c p e) k -> c p e k", p=P, e=TILES_PER_CHUNK)
         w2_view = W2.rearrange("(c s p) k -> c p s k", s=TILES_PER_CHUNK, p=P)
 
-        for r in range(ROW_BLOCKS):
+        chunk_tiles = []
+
+        def load_state(r):
             for cols in y_parts(r):
                 nc.sync.dma_start(out=h_sb[:, r, cols], in_=h_rows[:, r, cols])
                 nc.sync.dma_start(out=k3_sb[:, r, cols], in_=k3_rows[:, r, cols])
-        with nc.allow_non_contiguous_dma(reason="two bias vectors of 2 KiB, two values or one to a partition"):
-            nc.sync.dma_start(out=b1_cols[:], in_=b1.rearrange("(c p e) -> p c e", p=P, e=TILES_PER_CHUNK))
-            nc.sync.dma_start(out=b2_cols[:], in_=b2.rearrange("(s p) -> p s", p=P))
-        chunk_tiles = []
-        for c in range(CHUNKS):
+
+        def load_slopes(r):
+            nc.sync.dma_start(out=k2_sb[:, r, :], in_=k2_rows[:, r, :])
+            nc.sync.dma_start(out=k1_sb[:, r, :], in_=k1_rows[:, r, :])
+
+        def load_w1(c):
             w1_c = weights.tile([P, TILES_PER_CHUNK, W1_PITCH], BF16)
             nc.sync.dma_start(out=w1_c[:, :, 0 : H + 1], in_=w1_view[c])
             chunk_tiles.append(w1_c)
-            nc.sync.dma_start(out=k2_sb[:, c, :], in_=k2_rows[:, c, :])
-            nc.sync.dma_start(out=k1_sb[:, c, :], in_=k1_rows[:, c, :])
-        for c in range(CHUNKS):
+
+        def load_w2(c):
             w2_c = weights.tile([P, TILES_PER_CHUNK, H], BF16)
             nc.sync.dma_start(out=w2_c[:], in_=w2_view[c])
             chunk_tiles.append(w2_c)
+
+        def load_biases():
+            with nc.allow_non_contiguous_dma(reason="two bias vectors of 2 KiB, two values or one to a partition"):
+                nc.sync.dma_start(out=b1_cols[:], in_=b1.rearrange("(c p e) -> p c e", p=P, e=TILES_PER_CHUNK))
+                nc.sync.dma_start(out=b2_cols[:], in_=b2.rearrange("(s p) -> p s", p=P))
+
+        load_state(0)
+        load_state(1)
+        load_state(2)
+        load_state(3)
+        load_biases()
+        load_w1(0)
+        load_slopes(0)
+        load_w1(1)
+        load_slopes(1)
+        load_w1(2)
+        load_slopes(2)
+        load_w1(3)
+        load_slopes(3)
+        load_w2(0)
+        load_w2(1)
+        load_w2(2)
+        load_w2(3)
 
         ident_f32 = const.tile([P, P], F32)
         make_identity(nc, ident_f32[:])
@@ -144,7 +169,9 @@ def tile_nodelstmcell_pc_kernel(tc, h_tilde, k1, k2, k3, t0, t1, W1, b1, W2, b2,
         w_codes = keep.tile([P, 2, PASSES, H], U32, align_bytes=64)
         w_scales = keep.tile([P, 2, PASSES, H], U8, align_bytes=64)
         bias1 = const.tile([P, CHUNKS, TILES_PER_CHUNK], F32)
-        b2_all = const.tile([P, H], BF16)
+        b2_all = const.tile([P, N_HALF], BF16)
+        b2_left = const.tile([P, N_HALF // P], F32)
+        nc.scalar.copy(out=b2_left[:], in_=b2_cols[:, 0 : N_HALF // P])
         z_sb = keep.tile([P, H // P, B], BF16)
         z_grouped = keep.tile([P, PASSES, B * PACK], BF16, align_bytes=64)
         z_codes = keep.tile([P, PASSES, B], U32, align_bytes=64)
@@ -212,7 +239,8 @@ def tile_nodelstmcell_pc_kernel(tc, h_tilde, k1, k2, k3, t0, t1, W1, b1, W2, b2,
                 )
 
         def quantise_z(g):
-            nc.scalar.copy(
+            copy = nc.scalar.copy if g == 0 else nc.vector.tensor_copy
+            copy(
                 out=z_grouped[:, g, :].rearrange("p (c i t) -> p c t i", i=4, t=PACK),
                 in_=z_sb[:, PACK * g : PACK * (g + 1), :].rearrange("p t (c i) -> p c t i", i=4),
             )
@@ -224,7 +252,16 @@ def tile_nodelstmcell_pc_kernel(tc, h_tilde, k1, k2, k3, t0, t1, W1, b1, W2, b2,
             slopes = psum.tile([P, N_HALF], F32, tag="sum", bufs=2)
             nc.tensor.matmul(out=slopes[:], lhsT=ident_bf16[:], rhs=k1_sb[:, r, left], start=True, stop=False)
             nc.tensor.matmul(out=slopes[:], lhsT=twice_ident[:], rhs=k2_sb[:, r, left], start=False, stop=False)
-            nc.tensor.matmul(out=slopes[:], lhsT=twice_ident[:], rhs=k3_sb[:, r, left], start=False, stop=True)
+            nc.tensor.matmul(out=slopes[:], lhsT=twice_ident[:], rhs=k3_sb[:, r, left], start=False, stop=False)
+            for s in range(N_HALF // P):
+                nc.tensor.matmul(
+                    out=slopes[:, s * P : (s + 1) * P],
+                    lhsT=b2_left[:, s : s + 1].to_broadcast([P, P]),
+                    rhs=ident_f32[:],
+                    is_transpose=True,
+                    start=False,
+                    stop=(s == N_HALF // P - 1),
+                )
             slope_sums.append(slopes)
             nc.vector.tensor_tensor(out=base[:, r, right], in0=k2_sb[:, r, right], in1=k3_sb[:, r, right], op=ALU.add)
             nc.vector.scalar_tensor_tensor(
@@ -235,23 +272,24 @@ def tile_nodelstmcell_pc_kernel(tc, h_tilde, k1, k2, k3, t0, t1, W1, b1, W2, b2,
                 op0=ALU.mult,
                 op1=ALU.add,
             )
+            nc.vector.tensor_tensor(out=base[:, r, right], in0=base[:, r, right], in1=b2_all[:], op=ALU.add)
 
         def finish_base(r, cols, slopes):
-            nc.vector.tensor_tensor(out=base[:, r, cols], in0=slopes, in1=b2_all[:, cols], op=ALU.add)
             nc.vector.scalar_tensor_tensor(
                 out=base[:, r, cols],
-                in0=base[:, r, cols],
+                in0=slopes,
                 scalar=dt_sixth[:, 0:1],
                 in1=h_sb[:, r, cols],
                 op0=ALU.mult,
                 op1=ALU.add,
             )
 
-        b2_t = psum.tile([P, H], BF16, tag="tp")
-        for s in range(H // P):
+        b2_t = psum.tile([P, N_HALF], BF16, tag="tp")
+        for s in range(N_HALF // P):
+            column = N_HALF // P + s
             nc.tensor.transpose(
                 out=b2_t[:, s * P : (s + 1) * P],
-                in_=b2_cols[:, s : s + 1].to_broadcast([P, P]),
+                in_=b2_cols[:, column : column + 1].to_broadcast([P, P]),
                 identity=ident_bf16[:],
             )
         nc.scalar.copy(out=b2_all[:], in_=b2_t[:])

@@ -53,6 +53,11 @@ def tile_nodelstmcell_pc_kernel(tc, h_tilde, k1, k2, k3, t0, t1, W1, b1, W2, b2,
         nc.scalar.dma_start(out=t0_all[:], in_=t0.partition_broadcast(P))
         nc.scalar.dma_start(out=t1_all[:], in_=t1.partition_broadcast(P))
 
+        b1_rows = const.tile([P, CHUNK_ROWS], BF16)
+        b2_rows = const.tile([P, P], BF16)
+        nc.vector.memset(b1_rows[:], 0.0)
+        nc.vector.memset(b2_rows[:], 0.0)
+
         h_sb = data.tile([P, ROW_BLOCKS, H], BF16)
         k1_sb = data.tile([P, ROW_BLOCKS, H], BF16)
         k2_sb = data.tile([P, ROW_BLOCKS, H], BF16)
@@ -88,16 +93,12 @@ def tile_nodelstmcell_pc_kernel(tc, h_tilde, k1, k2, k3, t0, t1, W1, b1, W2, b2,
             nc.sync.dma_start(out=w2_c[:], in_=w2_view[c])
             chunk_tiles.append(w2_c)
 
-        def load_biases():
-            with nc.allow_non_contiguous_dma(reason="two bias vectors of 2 KiB, two values or one to a partition"):
-                nc.sync.dma_start(out=b1_cols[:], in_=b1.rearrange("(c p e) -> p c e", p=P, e=TILES_PER_CHUNK))
-                nc.sync.dma_start(out=b2_cols[:], in_=b2.rearrange("(s p) -> p s", p=P))
-
         load_state(0)
         load_state(1)
         load_state(2)
         load_state(3)
-        load_biases()
+        nc.sync.dma_start(out=b1_rows[0:CHUNKS, :], in_=b1.rearrange("(c w) -> c w", c=CHUNKS))
+        nc.sync.dma_start(out=b2_rows[0 : H // P, :], in_=b2.rearrange("(s p) -> s p", p=P))
         load_w1(0)
         load_slopes(0)
         load_w1(1)
@@ -171,7 +172,6 @@ def tile_nodelstmcell_pc_kernel(tc, h_tilde, k1, k2, k3, t0, t1, W1, b1, W2, b2,
         bias1 = const.tile([P, CHUNKS, TILES_PER_CHUNK], F32)
         b2_all = const.tile([P, N_HALF], BF16)
         b2_left = const.tile([P, N_HALF // P], F32)
-        nc.scalar.copy(out=b2_left[:], in_=b2_cols[:, 0 : N_HALF // P])
         z_sb = keep.tile([P, H // P, B], BF16)
         z_grouped = keep.tile([P, PASSES, B * PACK], BF16, align_bytes=64)
         z_codes = keep.tile([P, PASSES, B], U32, align_bytes=64)
@@ -283,6 +283,14 @@ def tile_nodelstmcell_pc_kernel(tc, h_tilde, k1, k2, k3, t0, t1, W1, b1, W2, b2,
                 op0=ALU.mult,
                 op1=ALU.add,
             )
+
+        b1_t = psum.tile([P, P], F32, tag="tp")
+        nc.tensor.transpose(out=b1_t[:], in_=b1_rows[:].bitcast(F32), identity=ident_f32[:])
+        nc.scalar.copy(out=b1_cols[:].rearrange("p c e -> p (c e)").bitcast(F32), in_=b1_t[:, 0:CHUNKS])
+        b2_cols_t = psum.tile([P, P], BF16, tag="tp")
+        nc.tensor.transpose(out=b2_cols_t[:], in_=b2_rows[:], identity=ident_bf16[:])
+        nc.scalar.copy(out=b2_cols[:], in_=b2_cols_t[:, 0 : H // P])
+        nc.scalar.copy(out=b2_left[:], in_=b2_cols[:, 0 : N_HALF // P])
 
         b2_t = psum.tile([P, N_HALF], BF16, tag="tp")
         for s in range(N_HALF // P):

@@ -28,6 +28,8 @@ HALVES = H // N_HALF
 QUANTISE_LAG = 1
 LAYER_LAG = 2
 Z_LAG = 3
+RIGHT_ROUNDS = (0, 2)
+FINISH_ROUNDS = (1, 4)
 
 FLOPS = 2 * 2 * B * H * H
 
@@ -62,26 +64,26 @@ def tile_nodelstmcell_pc_kernel(tc, h_tilde, k1, k2, k3, t0, t1, W1, b1, W2, b2,
         k1_sb = data.tile([P, ROW_BLOCKS, H], BF16)
         k2_sb = data.tile([P, ROW_BLOCKS, H], BF16)
         k3_sb = data.tile([P, ROW_BLOCKS, H], BF16)
-        h_rows = h_tilde.rearrange("(r p) j -> p r j", p=P)
-        k1_rows = k1.rearrange("(r p) j -> p r j", p=P)
-        k2_rows = k2.rearrange("(r p) j -> p r j", p=P)
-        k3_rows = k3.rearrange("(r p) j -> p r j", p=P)
-        out_rows = out.rearrange("(r p) j -> p r j", p=P)
+        h_rows = h_tilde.rearrange("(q p e) j -> p q e j", p=P, e=2)
+        k1_rows = k1.rearrange("(q p e) j -> p q e j", p=P, e=2)
+        k2_rows = k2.rearrange("(q p e) j -> p q e j", p=P, e=2)
+        k3_rows = k3.rearrange("(q p e) j -> p q e j", p=P, e=2)
+        out_rows = out.rearrange("(q p e) j -> p q e j", p=P, e=2)
         b1_cols = const.tile([P, CHUNKS, TILES_PER_CHUNK], BF16)
         b2_cols = const.tile([P, H // P], BF16)
         w1_view = W1.rearrange("(c p e) k -> c p e k", p=P, e=TILES_PER_CHUNK)
-        w2_view = W2.rearrange("(c s p) k -> c p s k", s=TILES_PER_CHUNK, p=P)
+        w2_view = W2.rearrange("(c p e) k -> c p e k", p=P, e=TILES_PER_CHUNK)
 
         chunk_tiles = []
 
         def load_state(r):
             for cols in y_parts(r):
-                nc.sync.dma_start(out=h_sb[:, r, cols], in_=h_rows[:, r, cols])
-                nc.sync.dma_start(out=k3_sb[:, r, cols], in_=k3_rows[:, r, cols])
+                nc.sync.dma_start(out=h_sb[:, r, cols], in_=h_rows[:, r // 2, r % 2, cols])
+                nc.sync.dma_start(out=k3_sb[:, r, cols], in_=k3_rows[:, r // 2, r % 2, cols])
 
-        def load_slopes(r):
-            nc.sync.dma_start(out=k2_sb[:, r, :], in_=k2_rows[:, r, :])
-            nc.sync.dma_start(out=k1_sb[:, r, :], in_=k1_rows[:, r, :])
+        def load_slopes(q):
+            nc.sync.dma_start(out=k2_sb[:, 2 * q : 2 * q + 2, :], in_=k2_rows[:, q, :, :])
+            nc.sync.dma_start(out=k1_sb[:, 2 * q : 2 * q + 2, :], in_=k1_rows[:, q, :, :])
 
         def load_w1(c):
             w1_c = weights.tile([P, TILES_PER_CHUNK, W1_PITCH], BF16)
@@ -96,17 +98,15 @@ def tile_nodelstmcell_pc_kernel(tc, h_tilde, k1, k2, k3, t0, t1, W1, b1, W2, b2,
         load_state(0)
         load_state(1)
         load_state(2)
-        load_state(3)
         nc.sync.dma_start(out=b1_rows[0:CHUNKS, :], in_=b1.rearrange("(c w) -> c w", c=CHUNKS))
         nc.sync.dma_start(out=b2_rows[0 : H // P, :], in_=b2.rearrange("(s p) -> s p", p=P))
-        load_w1(0)
+        load_state(3)
         load_slopes(0)
+        load_w1(0)
         load_w1(1)
-        load_slopes(1)
         load_w1(2)
-        load_slopes(2)
+        load_slopes(1)
         load_w1(3)
-        load_slopes(3)
         load_w2(0)
         load_w2(1)
         load_w2(2)
@@ -193,10 +193,16 @@ def tile_nodelstmcell_pc_kernel(tc, h_tilde, k1, k2, k3, t0, t1, W1, b1, W2, b2,
                             in_=w_words[:, s, first : first + P],
                             identity=ident_f32[:],
                         )
-                nc.scalar.copy(
-                    out=grouped[:, g, :].bitcast(F32).rearrange("p (c u) -> p c u", u=2),
-                    in_=w_t[:].rearrange("p u c -> p c u"),
-                )
+                if i < CHUNKS:
+                    nc.scalar.copy(
+                        out=grouped[:, g, :].bitcast(F32).rearrange("p (c u) -> p c u", u=2),
+                        in_=w_t[:].rearrange("p u c -> p c u"),
+                    )
+                else:
+                    nc.scalar.copy(
+                        out=grouped[:, g, :].bitcast(F32).rearrange("p (c e u) -> p c e u", e=TILES_PER_CHUNK, u=2),
+                        in_=w_t[:].rearrange("p u (e c) -> p c e u", e=TILES_PER_CHUNK),
+                    )
             grouped_tiles.append(grouped)
 
         def quantise_chunk(i):
@@ -248,7 +254,7 @@ def tile_nodelstmcell_pc_kernel(tc, h_tilde, k1, k2, k3, t0, t1, W1, b1, W2, b2,
                 out=z_codes[:, g, :].bitcast(FP8X4), scales=z_scales[:, g, :], in_=z_grouped[:, g, :]
             )
 
-        def add_slopes(r):
+        def add_left(r):
             slopes = psum.tile([P, N_HALF], F32, tag="sum", bufs=2)
             nc.tensor.matmul(out=slopes[:], lhsT=ident_bf16[:], rhs=k1_sb[:, r, left], start=True, stop=False)
             nc.tensor.matmul(out=slopes[:], lhsT=twice_ident[:], rhs=k2_sb[:, r, left], start=False, stop=False)
@@ -263,23 +269,35 @@ def tile_nodelstmcell_pc_kernel(tc, h_tilde, k1, k2, k3, t0, t1, W1, b1, W2, b2,
                     stop=(s == N_HALF // P - 1),
                 )
             slope_sums.append(slopes)
-            nc.vector.tensor_tensor(out=base[:, r, right], in0=k2_sb[:, r, right], in1=k3_sb[:, r, right], op=ALU.add)
+
+        def finish_left(r):
             nc.vector.scalar_tensor_tensor(
-                out=base[:, r, right],
-                in0=base[:, r, right],
-                scalar=2.0,
-                in1=k1_sb[:, r, right],
+                out=base[:, r, left],
+                in0=slope_sums[r][:],
+                scalar=dt_sixth[:, 0:1],
+                in1=h_sb[:, r, left],
                 op0=ALU.mult,
                 op1=ALU.add,
             )
-            nc.vector.tensor_tensor(out=base[:, r, right], in0=base[:, r, right], in1=b2_all[:], op=ALU.add)
 
-        def finish_base(r, cols, slopes):
+        def add_right(q):
+            two = slice(2 * q, 2 * q + 2)
+            sums = base[:, two, right]
+            nc.vector.tensor_tensor(out=sums, in0=k2_sb[:, two, right], in1=k3_sb[:, two, right], op=ALU.add)
             nc.vector.scalar_tensor_tensor(
-                out=base[:, r, cols],
-                in0=slopes,
+                out=sums, in0=sums, scalar=2.0, in1=k1_sb[:, two, right], op0=ALU.mult, op1=ALU.add
+            )
+            nc.vector.tensor_tensor(
+                out=sums, in0=sums, in1=b2_all[:].unsqueeze(1).to_broadcast([P, 2, N_HALF]), op=ALU.add
+            )
+
+        def finish_right(q):
+            two = slice(2 * q, 2 * q + 2)
+            nc.vector.scalar_tensor_tensor(
+                out=base[:, two, right],
+                in0=base[:, two, right],
                 scalar=dt_sixth[:, 0:1],
-                in1=h_sb[:, r, cols],
+                in1=h_sb[:, two, right],
                 op0=ALU.mult,
                 op1=ALU.add,
             )
@@ -309,15 +327,17 @@ def tile_nodelstmcell_pc_kernel(tc, h_tilde, k1, k2, k3, t0, t1, W1, b1, W2, b2,
                 quantise_chunk(i - QUANTISE_LAG)
             if 0 <= i - LAYER_LAG < CHUNKS:
                 first_layer(i - LAYER_LAG)
+            if i in RIGHT_ROUNDS:
+                add_right(RIGHT_ROUNDS.index(i))
             if i < ROW_BLOCKS:
-                add_slopes(i)
+                add_left(i)
             if 0 <= i - 1 < ROW_BLOCKS:
-                finish_base(i - 1, left, slope_sums[i - 1][:])
+                finish_left(i - 1)
             for g in range(PASSES):
                 if i - Z_LAG == 2 * g + 1:
                     quantise_z(g)
-            if 0 <= i - ROW_BLOCKS < ROW_BLOCKS:
-                finish_base(i - ROW_BLOCKS, right, base[:, i - ROW_BLOCKS, right])
+            if i in FINISH_ROUNDS:
+                finish_right(FINISH_ROUNDS.index(i))
 
         for half in range(HALVES):
             cols = slice(half * N_HALF, (half + 1) * N_HALF)
@@ -339,4 +359,4 @@ def tile_nodelstmcell_pc_kernel(tc, h_tilde, k1, k2, k3, t0, t1, W1, b1, W2, b2,
                         op0=ALU.mult,
                         op1=ALU.add,
                     )
-                    nc.sync.dma_start(out=out_rows[:, r, outer], in_=base[:, r, outer])
+                    nc.sync.dma_start(out=out_rows[:, r // 2, r % 2, outer], in_=base[:, r, outer])

@@ -256,9 +256,9 @@ def tile_nodelstmcell_pc_kernel(tc, h_tilde, k1, k2, k3, t0, t1, W1, b1, W2, b2,
 
         def add_left(r):
             slopes = psum.tile([P, N_HALF], F32, tag="sum", bufs=2)
-            nc.tensor.matmul(out=slopes[:], lhsT=ident_bf16[:], rhs=k1_sb[:, r, left], start=True, stop=False)
+            nc.tensor.matmul(out=slopes[:], lhsT=twice_ident[:], rhs=k3_sb[:, r, left], start=True, stop=False)
             nc.tensor.matmul(out=slopes[:], lhsT=twice_ident[:], rhs=k2_sb[:, r, left], start=False, stop=False)
-            nc.tensor.matmul(out=slopes[:], lhsT=twice_ident[:], rhs=k3_sb[:, r, left], start=False, stop=False)
+            nc.tensor.matmul(out=slopes[:], lhsT=ident_bf16[:], rhs=k1_sb[:, r, left], start=False, stop=False)
             for s in range(N_HALF // P):
                 nc.tensor.matmul(
                     out=slopes[:, s * P : (s + 1) * P],

from contextlib import ExitStack

import concourse.mybir as mybir
from concourse.masks import make_identity

F32 = mybir.dt.float32
BF16 = mybir.dt.bfloat16
U32 = mybir.dt.uint32
U8 = mybir.dt.uint8
FP8X4 = mybir.dt.float8_e4m3fn_x4
ALU = mybir.AluOpType
ACT = mybir.ActivationFunctionType

P = 128
B = 512
H = 1024
PACK = 4
K_PASS = P * PACK
PASSES = H // K_PASS
ROW_BLOCKS = B // P
CHUNKS = 4
CHUNK_ROWS = H // CHUNKS
TILES_PER_CHUNK = CHUNK_ROWS // P
WORDS = H // 2
W1_PITCH = H + 16
N_HALF = 512
HALVES = H // N_HALF
QUANTISE_LAG = 1
LAYER_LAG = 2
Z_LAG = 3
RIGHT_ROUNDS = (0, 2)
FINISH_ROUNDS = (1, 4)

FLOPS = 2 * 2 * B * H * H


def tile_nodelstmcell_pc_kernel(tc, h_tilde, k1, k2, k3, t0, t1, W1, b1, W2, b2, out):
    nc = tc.nc
    left = slice(0, N_HALF)
    right = slice(N_HALF, H)

    def y_parts(r):
        return (left, right) if r == 0 else (slice(0, H),)

    with ExitStack() as ctx:
        const = ctx.enter_context(tc.tile_pool(name="const", bufs=1))
        data = ctx.enter_context(tc.tile_pool(name="data", bufs=1))
        weights = ctx.enter_context(tc.tile_pool(name="weights", bufs=CHUNKS))
        stage = ctx.enter_context(tc.tile_pool(name="stage", bufs=3))
        keep = ctx.enter_context(tc.tile_pool(name="keep", bufs=1))
        psum = ctx.enter_context(tc.psum_pool(name="psum", bufs=3))

        t0_all = const.tile([P, 1], BF16)
        t1_all = const.tile([P, 1], BF16)
        nc.scalar.dma_start(out=t0_all[:], in_=t0.partition_broadcast(P))
        nc.scalar.dma_start(out=t1_all[:], in_=t1.partition_broadcast(P))

        b1_rows = const.tile([P, CHUNK_ROWS], BF16)
        b2_rows = const.tile([P, P], BF16)
        nc.vector.memset(b1_rows[:], 0.0)
        nc.vector.memset(b2_rows[:], 0.0)

        h_sb = data.tile([P, ROW_BLOCKS, H], BF16)
        k1_sb = data.tile([P, ROW_BLOCKS, H], BF16)
        k2_sb = data.tile([P, ROW_BLOCKS, H], BF16)
        k3_sb = data.tile([P, ROW_BLOCKS, H], BF16)
        h_rows = h_tilde.rearrange("(q p e) j -> p q e j", p=P, e=2)
        k1_rows = k1.rearrange("(q p e) j -> p q e j", p=P, e=2)
        k2_rows = k2.rearrange("(q p e) j -> p q e j", p=P, e=2)
        k3_rows = k3.rearrange("(q p e) j -> p q e j", p=P, e=2)
        out_rows = out.rearrange("(q p e) j -> p q e j", p=P, e=2)
        b1_cols = const.tile([P, CHUNKS, TILES_PER_CHUNK], BF16)
        b2_cols = const.tile([P, H // P], BF16)
        w1_view = W1.rearrange("(c p e) k -> c p e k", p=P, e=TILES_PER_CHUNK)
        w2_view = W2.rearrange("(c p e) k -> c p e k", p=P, e=TILES_PER_CHUNK)

        chunk_tiles = []

        def load_state(r):
            for cols in y_parts(r):
                nc.sync.dma_start(out=h_sb[:, r, cols], in_=h_rows[:, r // 2, r % 2, cols])
                nc.sync.dma_start(out=k3_sb[:, r, cols], in_=k3_rows[:, r // 2, r % 2, cols])

        def load_slopes(q):
            nc.sync.dma_start(out=k2_sb[:, 2 * q : 2 * q + 2, :], in_=k2_rows[:, q, :, :])
            nc.sync.dma_start(out=k1_sb[:, 2 * q : 2 * q + 2, :], in_=k1_rows[:, q, :, :])

        def load_w1(c):
            w1_c = weights.tile([P, TILES_PER_CHUNK, W1_PITCH], BF16)
            nc.sync.dma_start(out=w1_c[:, :, 0 : H + 1], in_=w1_view[c])
            chunk_tiles.append(w1_c)

        def load_w2(c):
            w2_c = weights.tile([P, TILES_PER_CHUNK, H], BF16)
            nc.sync.dma_start(out=w2_c[:], in_=w2_view[c])
            chunk_tiles.append(w2_c)

        load_state(0)
        load_state(1)
        load_state(2)
        nc.sync.dma_start(out=b1_rows[0:CHUNKS, :], in_=b1.rearrange("(c w) -> c w", c=CHUNKS))
        nc.sync.dma_start(out=b2_rows[0 : H // P, :], in_=b2.rearrange("(s p) -> s p", p=P))
        load_state(3)
        load_slopes(0)
        load_w1(0)
        load_w1(1)
        load_w1(2)
        load_slopes(1)
        load_w1(3)
        load_w2(0)
        load_w2(1)
        load_w2(2)
        load_w2(3)

        ident_f32 = const.tile([P, P], F32)
        make_identity(nc, ident_f32[:])
        ident_bf16 = const.tile([P, P], BF16)
        make_identity(nc, ident_bf16[:])
        warm_in = const.tile([P, 1], F32)
        warm_out = const.tile([P, 1], F32)
        nc.vector.memset(warm_in[:], 0.0)
        nc.scalar.activation(out=warm_out[:], in_=warm_in[:], func=ACT.Tanh)
        twice_ident = const.tile([P, P], BF16)
        nc.vector.tensor_scalar_mul(out=twice_ident[:], in0=ident_bf16[:], scalar1=2.0)

        dt = const.tile([P, 1], F32)
        t_end = const.tile([P, 1], F32)
        dt_sixth = const.tile([P, 1], F32)
        nc.vector.tensor_tensor(out=dt[:], in0=t1_all[:], in1=t0_all[:], op=ALU.subtract)
        nc.vector.tensor_tensor(out=t_end[:], in0=t0_all[:], in1=dt[:], op=ALU.add)
        nc.vector.tensor_scalar_mul(out=dt_sixth[:], in0=dt[:], scalar1=1.0 / 6.0)

        y_sb = keep.tile([P, ROW_BLOCKS, H], BF16)
        y_grouped = keep.tile([P, PASSES, B, PACK], BF16, align_bytes=64)
        y_codes = keep.tile([P, PASSES, B], U32, align_bytes=64)
        y_scales = keep.tile([P, PASSES, B], U8, align_bytes=64)
        for r in range(ROW_BLOCKS):
            for cols in y_parts(r):
                nc.vector.scalar_tensor_tensor(
                    out=y_sb[:, r, cols],
                    in0=k3_sb[:, r, cols],
                    scalar=dt[:, 0:1],
                    in1=h_sb[:, r, cols],
                    op0=ALU.mult,
                    op1=ALU.add,
                )
            y_words = y_sb[:, r, :].bitcast(F32)
            y_t = psum.tile([P, PASSES, 2, P], F32, tag="tp")
            for g in range(PASSES):
                for u in range(2):
                    first = (2 * g + u) * P
                    nc.tensor.transpose(
                        out=y_t[:, g, u, :],
                        in_=y_words[:, first : first + P],
                        identity=ident_f32[:],
                    )
            nc.scalar.copy(
                out=y_grouped[:, :, r * P : (r + 1) * P, :]
                .rearrange("p g b t -> p g (b t)")
                .bitcast(F32)
                .rearrange("p g (b u) -> p g b u", u=2),
                in_=y_t[:].rearrange("p g u b -> p g b u"),
            )
        nc.vector.quantize_mx(
            out=y_codes[:].rearrange("p g b -> p (g b)").bitcast(FP8X4),
            scales=y_scales[:].rearrange("p g b -> p (g b)"),
            in_=y_grouped[:].rearrange("p g b t -> p (g b t)"),
        )

        w_codes = keep.tile([P, 2, PASSES, H], U32, align_bytes=64)
        w_scales = keep.tile([P, 2, PASSES, H], U8, align_bytes=64)
        bias1 = const.tile([P, CHUNKS, TILES_PER_CHUNK], F32)
        b2_all = const.tile([P, N_HALF], BF16)
        b2_left = const.tile([P, N_HALF // P], F32)
        z_sb = keep.tile([P, H // P, B], BF16)
        z_grouped = keep.tile([P, PASSES, B * PACK], BF16, align_bytes=64)
        z_codes = keep.tile([P, PASSES, B], U32, align_bytes=64)
        z_scales = keep.tile([P, PASSES, B], U8, align_bytes=64)
        base = keep.tile([P, ROW_BLOCKS, H], F32)
        grouped_tiles = []
        slope_sums = []

        def transpose_chunk(i):
            w_words = chunk_tiles[i][:].bitcast(F32)
            grouped = stage.tile([P, PASSES, CHUNK_ROWS * PACK], BF16, align_bytes=64)
            for g in range(PASSES):
                w_t = psum.tile([P, 2, CHUNK_ROWS], F32, tag="tp")
                for u in range(2):
                    for s in range(TILES_PER_CHUNK):
                        first = (2 * g + u) * P
                        nc.tensor.transpose(
                            out=w_t[:, u, s * P : (s + 1) * P],
                            in_=w_words[:, s, first : first + P],
                            identity=ident_f32[:],
                        )
                if i < CHUNKS:
                    nc.scalar.copy(
                        out=grouped[:, g, :].bitcast(F32).rearrange("p (c u) -> p c u", u=2),
                        in_=w_t[:].rearrange("p u c -> p c u"),
                    )
                else:
                    nc.scalar.copy(
                        out=grouped[:, g, :].bitcast(F32).rearrange("p (c e u) -> p c e u", e=TILES_PER_CHUNK, u=2),
                        in_=w_t[:].rearrange("p u (e c) -> p c e u", e=TILES_PER_CHUNK),
                    )
            grouped_tiles.append(grouped)

        def quantise_chunk(i):
            rows = slice((i % CHUNKS) * CHUNK_ROWS, (i % CHUNKS + 1) * CHUNK_ROWS)
            for g in range(PASSES):
                nc.vector.quantize_mx(
                    out=w_codes[:, i // CHUNKS, g, rows].bitcast(FP8X4),
                    scales=w_scales[:, i // CHUNKS, g, rows],
                    in_=grouped_tiles[i][:, g, :],
                )

        def multiply(still_codes, still_scales, moving_codes, moving_scales):
            acc = psum.tile([P, N_HALF], F32, tag="acc")
            for g in range(PASSES):
                nc.tensor.matmul_mx(
                    out=acc[:],
                    lhsT=still_codes[:, g, :].bitcast(FP8X4),
                    lhsT_scale=still_scales[:, g, :],
                    rhs=moving_codes[:, g, :].bitcast(FP8X4),
                    rhs_scale=moving_scales[:, g, :],
                    start=(g == 0),
                    stop=(g == PASSES - 1),
                )
            return acc

        def first_layer(c):
            nc.gpsimd.tensor_scalar(
                out=bias1[:, c, :], in0=chunk_tiles[c][:, :, H], scalar1=t_end[:, 0:1], scalar2=None, op0=ALU.mult
            )
            nc.gpsimd.tensor_tensor(out=bias1[:, c, :], in0=bias1[:, c, :], in1=b1_cols[:, c, :], op=ALU.add)
            for e in range(TILES_PER_CHUNK):
                rows = slice((TILES_PER_CHUNK * c + e) * P, (TILES_PER_CHUNK * c + e + 1) * P)
                acc = multiply(w_codes[:, 0, :, rows], w_scales[:, 0, :, rows], y_codes, y_scales)
                nc.scalar.activation(
                    out=z_sb[:, TILES_PER_CHUNK * c + e, :],
                    in_=acc[:],
                    func=ACT.Tanh,
                    bias=bias1[:, c, e : e + 1],
                    scale=1.0,
                )

        def quantise_z(g):
            copy = nc.scalar.copy if g == 0 else nc.vector.tensor_copy
            copy(
                out=z_grouped[:, g, :].rearrange("p (c i t) -> p c t i", i=4, t=PACK),
                in_=z_sb[:, PACK * g : PACK * (g + 1), :].rearrange("p t (c i) -> p c t i", i=4),
            )
            nc.vector.quantize_mx(
                out=z_codes[:, g, :].bitcast(FP8X4), scales=z_scales[:, g, :], in_=z_grouped[:, g, :]
            )

        def add_left(r):
            slopes = psum.tile([P, N_HALF], F32, tag="sum", bufs=2)
            nc.tensor.matmul(out=slopes[:], lhsT=twice_ident[:], rhs=k3_sb[:, r, left], start=True, stop=False)
            nc.tensor.matmul(out=slopes[:], lhsT=twice_ident[:], rhs=k2_sb[:, r, left], start=False, stop=False)
            nc.tensor.matmul(out=slopes[:], lhsT=ident_bf16[:], rhs=k1_sb[:, r, left], start=False, stop=False)
            for s in range(N_HALF // P):
                nc.tensor.matmul(
                    out=slopes[:, s * P : (s + 1) * P],
                    lhsT=b2_left[:, s : s + 1].to_broadcast([P, P]),
                    rhs=ident_f32[:],
                    is_transpose=True,
                    start=False,
                    stop=(s == N_HALF // P - 1),
                )
            slope_sums.append(slopes)

        def finish_left(r):
            nc.vector.scalar_tensor_tensor(
                out=base[:, r, left],
                in0=slope_sums[r][:],
                scalar=dt_sixth[:, 0:1],
                in1=h_sb[:, r, left],
                op0=ALU.mult,
                op1=ALU.add,
            )

        def add_right(q):
            two = slice(2 * q, 2 * q + 2)
            sums = base[:, two, right]
            nc.vector.tensor_tensor(out=sums, in0=k2_sb[:, two, right], in1=k3_sb[:, two, right], op=ALU.add)
            nc.vector.scalar_tensor_tensor(
                out=sums, in0=sums, scalar=2.0, in1=k1_sb[:, two, right], op0=ALU.mult, op1=ALU.add
            )
            nc.vector.tensor_tensor(
                out=sums, in0=sums, in1=b2_all[:].unsqueeze(1).to_broadcast([P, 2, N_HALF]), op=ALU.add
            )

        def finish_right(q):
            two = slice(2 * q, 2 * q + 2)
            nc.vector.scalar_tensor_tensor(
                out=base[:, two, right],
                in0=base[:, two, right],
                scalar=dt_sixth[:, 0:1],
                in1=h_sb[:, two, right],
                op0=ALU.mult,
                op1=ALU.add,
            )

        b1_t = psum.tile([P, P], F32, tag="tp")
        nc.tensor.transpose(out=b1_t[:], in_=b1_rows[:].bitcast(F32), identity=ident_f32[:])
        nc.scalar.copy(out=b1_cols[:].rearrange("p c e -> p (c e)").bitcast(F32), in_=b1_t[:, 0:CHUNKS])
        b2_cols_t = psum.tile([P, P], BF16, tag="tp")
        nc.tensor.transpose(out=b2_cols_t[:], in_=b2_rows[:], identity=ident_bf16[:])
        nc.scalar.copy(out=b2_cols[:], in_=b2_cols_t[:, 0 : H // P])
        nc.scalar.copy(out=b2_left[:], in_=b2_cols[:, 0 : N_HALF // P])

        b2_t = psum.tile([P, N_HALF], BF16, tag="tp")
        for s in range(N_HALF // P):
            column = N_HALF // P + s
            nc.tensor.transpose(
                out=b2_t[:, s * P : (s + 1) * P],
                in_=b2_cols[:, column : column + 1].to_broadcast([P, P]),
                identity=ident_bf16[:],
            )
        nc.scalar.copy(out=b2_all[:], in_=b2_t[:])

        for i in range(2 * CHUNKS + QUANTISE_LAG):
            if i < 2 * CHUNKS:
                transpose_chunk(i)
            if i >= QUANTISE_LAG:
                quantise_chunk(i - QUANTISE_LAG)
            if 0 <= i - LAYER_LAG < CHUNKS:
                first_layer(i - LAYER_LAG)
            if i in RIGHT_ROUNDS:
                add_right(RIGHT_ROUNDS.index(i))
            if i < ROW_BLOCKS:
                add_left(i)
            if 0 <= i - 1 < ROW_BLOCKS:
                finish_left(i - 1)
            for g in range(PASSES):
                if i - Z_LAG == 2 * g + 1:
                    quantise_z(g)
            if i in FINISH_ROUNDS:
                finish_right(FINISH_ROUNDS.index(i))

        for half in range(HALVES):
            cols = slice(half * N_HALF, (half + 1) * N_HALF)
            for r in range(ROW_BLOCKS):
                batch = slice(r * P, (r + 1) * P)
                acc = multiply(
                    z_codes[:, :, batch], z_scales[:, :, batch], w_codes[:, 1, :, cols], w_scales[:, 1, :, cols]
                )
                parts = 2 if half == HALVES - 1 and r == ROW_BLOCKS - 1 else 1
                width = N_HALF // parts
                for part in range(parts):
                    inner = slice(part * width, (part + 1) * width)
                    outer = slice(half * N_HALF + part * width, half * N_HALF + (part + 1) * width)
                    nc.vector.scalar_tensor_tensor(
                        out=base[:, r, outer],
                        in0=acc[:, inner],
                        scalar=dt_sixth[:, 0:1],
                        in1=base[:, r, outer],
                        op0=ALU.mult,
                        op1=ALU.add,
                    )
                    nc.sync.dma_start(out=out_rows[:, r // 2, r % 2, outer], in_=base[:, r, outer])
